import numpy as np
import ml_dtypes


def mxq(x, axis, fmt="e4m3"):
    dtype, down = {"e4m3": (ml_dtypes.float8_e4m3fn, 7), "e5m2": (ml_dtypes.float8_e5m2, 14)}[fmt]
    v = np.moveaxis(np.asarray(x, np.float32).astype(ml_dtypes.bfloat16).astype(np.float64), axis, -1)
    blocks = v.reshape(v.shape[:-1] + (-1, 32))
    amax = np.abs(blocks).max(-1, keepdims=True)
    byte = np.maximum(np.where(amax > 0, np.frexp(amax)[1] - 1 + 127, 0) - down, 1)
    scale = np.exp2(byte - 127.0)
    codes = (blocks / scale).astype(np.float32).astype(dtype).astype(np.float64)
    return np.moveaxis((codes * scale).reshape(v.shape), -1, axis)


WIDE = False


def mx_kscale(k):
    if not WIDE:
        return np.ones(k)
    levels = np.array([10, -10, 5, -5, 0])
    if k % 512:
        return np.exp2(np.random.permutation(np.resize(levels, k // 32))).repeat(32)
    a = np.empty((k // 512, 16))
    for p in range(k // 512):
        a[p, :8] = np.random.permutation(np.resize(levels, 8))
        for g in range(8):
            far = levels[np.abs(levels - a[p, g]) >= 10]
            a[p, g + 8] = far[np.random.randint(len(far))]
    return np.exp2(a.ravel()).repeat(32)


BF16 = ml_dtypes.bfloat16


def bf(x):
    return np.asarray(x, np.float32).astype(BF16)


def f64(x):
    return np.asarray(x).astype(np.float64)


B, S, D, DM, DK = 4, 1024, 512, 1024, 64
LN_EPS = 1e-5


def setup_inputs():
    s = mx_kscale(DM)
    return {
        "h_attn": bf(np.random.standard_normal((B, S, DM)) * 0.3 * s),
        "Wo": bf(np.random.standard_normal((DM, D)) * 3.0 / np.sqrt(DM) / s[:, None]),
        "bo": bf(np.random.standard_normal((B, S, D)) * 0.5 + np.random.uniform(0.25, 0.75, (B, 1, 1))),
        "x": bf(np.random.standard_normal((B, S, D))),
        "gamma": bf(1.0 + 0.1 * np.random.standard_normal((S, D))),
        "beta": bf(0.1 * np.random.standard_normal((S, D))),
    }


def reference(h_attn, Wo, bo, x, gamma, beta):
    o = (mxq(f64(h_attn), 2, "e4m3") @ mxq(f64(Wo), 0, "e4m3")) + f64(bo)
    o = o + f64(x)
    mu = o.mean(axis=(-2, -1), keepdims=True)
    var = np.square(o - mu).mean(axis=(-2, -1), keepdims=True)
    return (o - mu) / np.sqrt(var + LN_EPS) * f64(gamma) + f64(beta)

@@ -1,0 +1,289 @@
+from contextlib import ExitStack
+
+import concourse.mybir as mybir
+from concourse.masks import make_identity
+
+F32 = mybir.dt.float32
+BF16 = mybir.dt.bfloat16
+U32 = mybir.dt.uint32
+U8 = mybir.dt.uint8
+FP8X4 = mybir.dt.float8_e4m3fn_x4
+ADD = mybir.AluOpType.add
+MULT = mybir.AluOpType.mult
+FUNC = mybir.ActivationFunctionType
+
+P = 128
+BATCH, SEQ, K_DIM, D_OUT = 4, 1024, 1024, 512
+LN_EPS = 1e-5
+PACK = 4
+K_PASS = P * PACK
+PASSES = K_DIM // K_PASS
+TILES_PER_BATCH = SEQ // P
+CHUNK_TILES = 4
+CHUNKS_PER_BATCH = TILES_PER_BATCH // CHUNK_TILES
+CHUNKS = BATCH * CHUNKS_PER_BATCH
+CHUNK_K = CHUNK_TILES * K_DIM
+CHUNK_D = CHUNK_TILES * D_OUT
+BATCH_D = TILES_PER_BATCH * D_OUT
+WORDS = K_DIM // 2
+PLANES = WORDS // P
+TILE_CODES = K_DIM // PACK
+NORM_PIECES = 2
+PIECE_D = CHUNK_D // NORM_PIECES
+COUNT = SEQ * D_OUT
+
+INPUT_BUFS = 4
+STAGE_BUFS = 3
+
+TENSOR_ADD_FROM = CHUNKS // 2
+TENSOR_ADD_TILES = 3
+GPSIMD_ADD_FROM = 3
+assert GPSIMD_ADD_FROM <= TENSOR_ADD_FROM
+
+FLOPS = 2 * BATCH * SEQ * K_DIM * D_OUT
+
+
+def tile_multiheadattn_pb_t_kernel(tc, h_attn, Wo, bo, x, gamma, beta, out):
+    nc = tc.nc
+
+    h_view = h_attn.rearrange("b (p t) k -> p b (t k)", t=TILES_PER_BATCH)
+    bo_view = bo.rearrange("b (p t) d -> p b (t d)", t=TILES_PER_BATCH)
+    x_view = x.rearrange("b (p t) d -> p b (t d)", t=TILES_PER_BATCH)
+    out_view = out.rearrange("b (p t) d -> p b (t d)", t=TILES_PER_BATCH)
+    gamma_view = gamma.rearrange("(p t) d -> p (t d)", t=TILES_PER_BATCH)
+    beta_view = beta.rearrange("(p t) d -> p (t d)", t=TILES_PER_BATCH)
+    wo_view = Wo.rearrange("(g q t) c -> q g (t c)", g=PASSES, t=PACK)
+
+    with ExitStack() as ctx:
+        const = ctx.enter_context(tc.tile_pool(name="const", bufs=1))
+        h_pool = ctx.enter_context(tc.tile_pool(name="h_pool", bufs=INPUT_BUFS))
+        add_pool = ctx.enter_context(tc.tile_pool(name="add_pool", bufs=INPUT_BUFS))
+        grouped_pool = ctx.enter_context(tc.tile_pool(name="grouped_pool", bufs=STAGE_BUFS))
+        mx_pool = ctx.enter_context(tc.tile_pool(name="mx_pool", bufs=STAGE_BUFS))
+        scratch_pool = ctx.enter_context(tc.tile_pool(name="scratch_pool", bufs=4))
+        psum_xt = ctx.enter_context(tc.psum_pool(name="psum_xt", bufs=2))
+        psum_acc = ctx.enter_context(tc.psum_pool(name="psum_acc", bufs=CHUNK_TILES))
+        psum_plain = ctx.enter_context(tc.psum_pool(name="psum_plain", bufs=2))
+
+        ident = const.tile([P, P], F32)
+        make_identity(nc, ident[:])
+        ident_bf16 = const.tile([P, P], BF16)
+        make_identity(nc, ident_bf16[:])
+        ones = const.tile([P, P], F32)
+        nc.vector.memset(ones[:], 1.0)
+        eps = const.tile([P, 1], F32)
+        nc.vector.memset(eps[:], LN_EPS)
+
+        tile_sums = const.tile([P, BATCH * TILES_PER_BATCH], F32)
+        neg_mean = const.tile([P, BATCH], F32)
+        mean_scratch = const.tile([P, BATCH * TILES_PER_BATCH], F32)
+        square_sums = const.tile([P, BATCH * TILES_PER_BATCH], F32)
+        var_scratch = const.tile([P, BATCH * TILES_PER_BATCH], F32)
+        var = const.tile([P, BATCH], F32)
+        std = const.tile([P, BATCH], F32)
+        rstd = const.tile([P, BATCH], F32)
+
+        o_tiles = [const.tile([P, BATCH_D], F32, name="o%d" % b) for b in range(BATCH)]
+        gamma_sb = const.tile([P, BATCH_D], BF16)
+        beta_sb = const.tile([P, BATCH_D], BF16)
+
+        wo_raw = const.tile([P, PASSES * PACK * D_OUT], BF16)
+        wo_grouped = const.tile([P, PASSES * D_OUT * PACK], BF16, align_bytes=64)
+        wo_codes = const.tile([P, PASSES * D_OUT], U32, align_bytes=64)
+        wo_scales = const.tile([P, PASSES * D_OUT], U8, align_bytes=64)
+        wo_raw_passes = wo_raw[:].rearrange("q (g r) -> q g r", g=PASSES)
+        for g in range(PASSES):
+            nc.sync.dma_start(out=wo_raw_passes[:, g, :], in_=wo_view[:, g, :])
+        wo_raw_gct = wo_raw[:].rearrange("q (g t c) -> q g c t", g=PASSES, t=PACK)
+        wo_grouped_gct = wo_grouped[:].rearrange("q (g c t) -> q g c t", g=PASSES, t=PACK)
+        for g in range(PASSES):
+            nc.vector.tensor_copy(out=wo_grouped_gct[:, g], in_=wo_raw_gct[:, g])
+        for g in range(PASSES):
+            nc.vector.quantize_mx(
+                out=wo_codes[:, g * D_OUT : (g + 1) * D_OUT].bitcast(FP8X4),
+                scales=wo_scales[:, g * D_OUT : (g + 1) * D_OUT],
+                in_=wo_grouped[:, g * D_OUT * PACK : (g + 1) * D_OUT * PACK],
+            )
+
+        h_in, bo_in, x_in = {}, {}, {}
+        h_grouped, h_codes, h_scales = {}, {}, {}
+        acc_of = {}
+
+        def chunk_cols(c, width):
+            half = c % CHUNKS_PER_BATCH
+            return slice(half * width, (half + 1) * width)
+
+        def load(c):
+            b = c // CHUNKS_PER_BATCH
+            h_sb = h_pool.tile([P, CHUNK_K], BF16)
+            nc.sync.dma_start(out=h_sb[:], in_=h_view[:, b, chunk_cols(c, CHUNK_K)])
+            bo_sb = add_pool.tile([P, CHUNK_D], BF16)
+            nc.sync.dma_start(out=bo_sb[:], in_=bo_view[:, b, chunk_cols(c, CHUNK_D)])
+            x_sb = add_pool.tile([P, CHUNK_D], BF16)
+            nc.sync.dma_start(out=x_sb[:], in_=x_view[:, b, chunk_cols(c, CHUNK_D)])
+            h_in[c], bo_in[c], x_in[c] = h_sb, bo_sb, x_sb
+
+        def transpose(c):
+            h_words = h_in[c][:].bitcast(F32)
+            grouped = grouped_pool.tile([P, CHUNK_K], BF16, align_bytes=64)
+            grouped_words = grouped[:].bitcast(F32)
+            for j in range(CHUNK_TILES):
+                xt = psum_xt.tile([P, PLANES, P], F32)
+                for a in range(PLANES):
+                    g, u = divmod(a, 2)
+                    first = j * WORDS + 2 * g * P
+                    nc.tensor.transpose(xt[:, a, :], h_words[:, first + u : first + 2 * P : 2], ident[:])
+                nc.scalar.copy(
+                    out=grouped_words[:, j * WORDS : (j + 1) * WORDS].rearrange(
+                        "q (g r u) -> q g r u", g=PASSES, u=2
+                    ),
+                    in_=xt[:].rearrange("q (g u) r -> q g r u", g=PASSES),
+                )
+            h_grouped[c] = grouped
+
+        def quantise(c):
+            codes = mx_pool.tile([P, CHUNK_TILES * TILE_CODES], U32, align_bytes=64)
+            scales = mx_pool.tile([P, CHUNK_TILES * TILE_CODES], U8, align_bytes=64)
+            nc.vector.quantize_mx(
+                out=codes[:].bitcast(FP8X4), scales=scales[:], in_=h_grouped[c][:]
+            )
+            h_codes[c], h_scales[c] = codes, scales
+
+        def project(c):
+            for j in range(CHUNK_TILES):
+                acc = psum_acc.tile([P, D_OUT], F32)
+                for g in range(PASSES):
+                    tokens = slice((j * PASSES + g) * P, (j * PASSES + g + 1) * P)
+                    features = slice(g * D_OUT, (g + 1) * D_OUT)
+                    nc.tensor.matmul_mx(
+                        out=acc[:],
+                        lhsT=h_codes[c][:, tokens].bitcast(FP8X4),
+                        lhsT_scale=h_scales[c][:, tokens],
+                        rhs=wo_codes[:, features].bitcast(FP8X4),
+                        rhs_scale=wo_scales[:, features],
+                        start=(g == 0),
+                        stop=(g == PASSES - 1),
+                    )
+                acc_of[(c, j)] = acc
+
+        def add_bias_and_residual(c):
+            o_chunk = o_tiles[c // CHUNKS_PER_BATCH][:, chunk_cols(c, CHUNK_D)]
+            plain_tiles = CHUNK_TILES if c < TENSOR_ADD_FROM else CHUNK_TILES - TENSOR_ADD_TILES
+            if c < GPSIMD_ADD_FROM:
+                nc.vector.tensor_tensor(out=o_chunk, in0=bo_in[c][:], in1=x_in[c][:], op=ADD)
+            else:
+                for j in range(plain_tiles):
+                    cols = slice(j * D_OUT, (j + 1) * D_OUT)
+                    nc.gpsimd.tensor_tensor(
+                        out=o_chunk[:, cols], in0=bo_in[c][:, cols], in1=x_in[c][:, cols], op=ADD
+                    )
+            for j in range(plain_tiles, CHUNK_TILES):
+                cols = slice(j * D_OUT, (j + 1) * D_OUT)
+                bx = psum_plain.tile([P, D_OUT], F32, tag="plain")
+                nc.tensor.matmul(bx[:], lhsT=ident_bf16[:], rhs=bo_in[c][:, cols], start=True, stop=False)
+                nc.tensor.matmul(bx[:], lhsT=ident_bf16[:], rhs=x_in[c][:, cols], start=False, stop=True)
+                nc.scalar.copy(out=o_chunk[:, cols], in_=bx[:])
+
+        def add_projection(c):
+            o_chunk = o_tiles[c // CHUNKS_PER_BATCH][:, chunk_cols(c, CHUNK_D)]
+            for j in range(CHUNK_TILES):
+                o_tile = o_chunk[:, j * D_OUT : (j + 1) * D_OUT]
+                column = c * CHUNK_TILES + j
+                nc.vector.scalar_tensor_tensor(
+                    out=o_tile,
+                    in0=acc_of[(c, j)][:],
+                    scalar=0.0,
+                    in1=o_tile,
+                    op0=ADD,
+                    op1=ADD,
+                    accum_out=tile_sums[:, column : column + 1],
+                )
+
+        def mean(b):
+            columns = slice(b * TILES_PER_BATCH, (b + 1) * TILES_PER_BATCH)
+            totals = psum_plain.tile([P, TILES_PER_BATCH], F32, tag="plain")
+            nc.tensor.matmul(totals[:], lhsT=ones[:], rhs=tile_sums[:, columns], start=True, stop=True)
+            nc.scalar.activation(
+                out=mean_scratch[:, columns],
+                in_=totals[:],
+                func=FUNC.Copy,
+                scale=-1.0 / COUNT,
+                accum_out=neg_mean[:, b : b + 1],
+            )
+
+        def square_tile(c, j):
+            b = c // CHUNKS_PER_BATCH
+            first = (c % CHUNKS_PER_BATCH) * CHUNK_D + j * D_OUT
+            column = c * CHUNK_TILES + j
+            squares = scratch_pool.tile([P, D_OUT], BF16)
+            nc.scalar.activation(
+                out=squares[:],
+                in_=o_tiles[b][:, first : first + D_OUT],
+                func=FUNC.Square,
+                bias=neg_mean[:, b : b + 1],
+                accum_out=square_sums[:, column : column + 1],
+            )
+
+        def standard_deviation(b):
+            columns = slice(b * TILES_PER_BATCH, (b + 1) * TILES_PER_BATCH)
+            totals = psum_plain.tile([P, TILES_PER_BATCH], F32, tag="plain")
+            nc.tensor.matmul(totals[:], lhsT=ones[:], rhs=square_sums[:, columns], start=True, stop=True)
+            nc.scalar.activation(
+                out=var_scratch[:, columns],
+                in_=totals[:],
+                func=FUNC.Copy,
+                scale=1.0 / COUNT,
+                accum_out=var[:, b : b + 1],
+            )
+            nc.scalar.activation(out=std[:, b : b + 1], in_=var[:, b : b + 1], func=FUNC.Sqrt, bias=eps[:])
+
+        def normalise_and_store(c):
+            b = c // CHUNKS_PER_BATCH
+            if c % CHUNKS_PER_BATCH == 0:
+                nc.vector.reciprocal(out=rstd[:, b : b + 1], in_=std[:, b : b + 1])
+            first = (c % CHUNKS_PER_BATCH) * CHUNK_D
+            pieces = [slice(first + n * PIECE_D, first + (n + 1) * PIECE_D) for n in range(NORM_PIECES)]
+            for piece in pieces:
+                nc.vector.scalar_tensor_tensor(
+                    out=o_tiles[b][:, piece],
+                    in0=o_tiles[b][:, piece],
+                    scalar=neg_mean[:, b : b + 1],
+                    in1=gamma_sb[:, piece],
+                    op0=ADD,
+                    op1=MULT,
+                )
+            for piece in pieces:
+                nc.vector.scalar_tensor_tensor(
+                    out=o_tiles[b][:, piece],
+                    in0=o_tiles[b][:, piece],
+                    scalar=rstd[:, b : b + 1],
+                    in1=beta_sb[:, piece],
+                    op0=MULT,
+                    op1=ADD,
+                )
+                nc.sync.dma_start(out=out_view[:, b, piece], in_=o_tiles[b][:, piece])
+
+        def is_chunk(c):
+            return 0 <= c < CHUNKS
+
+        for c in range(INPUT_BUFS):
+            load(c)
+        nc.sync.dma_start(out=gamma_sb[:], in_=gamma_view)
+        nc.sync.dma_start(out=beta_sb[:], in_=beta_view)
+        for c in range(CHUNKS):
+            transpose(c)
+            quantise(c)
+            add_bias_and_residual(c)
+            project(c)
+            add_projection(c)
+            if is_chunk(c + INPUT_BUFS):
+                load(c + INPUT_BUFS)
+            if c % CHUNKS_PER_BATCH == CHUNKS_PER_BATCH - 1:
+                b = c // CHUNKS_PER_BATCH
+                mean(b)
+                for cc in range(c - CHUNKS_PER_BATCH + 1, c + 1):
+                    for j in range(CHUNK_TILES):
+                        square_tile(cc, j)
+                standard_deviation(b)
+        for c in range(CHUNKS):
+            normalise_and_store(c)

@@ -28,17 +28,20 @@ BATCH_D = TILES_PER_BATCH * D_OUT
 WORDS = K_DIM // 2
 PLANES = WORDS // P
 TILE_CODES = K_DIM // PACK
-NORM_PIECES = 2
-PIECE_D = CHUNK_D // NORM_PIECES
+HALF_TILES = CHUNK_TILES // 2
+PIECES = 4
+PIECE_D = BATCH_D // PIECES
+PIECES_PER_STEP = PIECES // CHUNKS_PER_BATCH
 COUNT = SEQ * D_OUT
 
-INPUT_BUFS = 4
+INPUT_BUFS = 5
 STAGE_BUFS = 3
 
 TENSOR_ADD_FROM = CHUNKS // 2
 TENSOR_ADD_TILES = 3
-GPSIMD_ADD_FROM = 3
-assert GPSIMD_ADD_FROM <= TENSOR_ADD_FROM
+ALL_TILES = slice(0, CHUNK_TILES)
+FIRST_HALF = slice(0, HALF_TILES)
+SECOND_HALF = slice(HALF_TILES, CHUNK_TILES)
 
 FLOPS = 2 * BATCH * SEQ * K_DIM * D_OUT
 
@@ -71,15 +74,16 @@ def tile_multiheadattn_pb_t_kernel(tc, h_attn, Wo, bo, x, gamma, beta, out):
         make_identity(nc, ident_bf16[:])
         ones = const.tile([P, P], F32)
         nc.vector.memset(ones[:], 1.0)
-        eps = const.tile([P, 1], F32)
-        nc.vector.memset(eps[:], LN_EPS)
+        eps_part = const.tile([P, 1], F32)
+        nc.vector.memset(eps_part[:], LN_EPS / TILES_PER_BATCH)
 
-        tile_sums = const.tile([P, BATCH * TILES_PER_BATCH], F32)
+        STATS = 2 * TILES_PER_BATCH
+        stats = const.tile([P, BATCH * STATS], F32)
+        scratch = const.tile([P, BATCH * STATS], F32)
+        neg_shift = const.tile([P, BATCH], F32)
         neg_mean = const.tile([P, BATCH], F32)
-        mean_scratch = const.tile([P, BATCH * TILES_PER_BATCH], F32)
-        square_sums = const.tile([P, BATCH * TILES_PER_BATCH], F32)
-        var_scratch = const.tile([P, BATCH * TILES_PER_BATCH], F32)
-        var = const.tile([P, BATCH], F32)
+        mean_square = const.tile([P, BATCH], F32)
+        gap_square = const.tile([P, BATCH], F32)
         std = const.tile([P, BATCH], F32)
         rstd = const.tile([P, BATCH], F32)
 
@@ -92,13 +96,16 @@ def tile_multiheadattn_pb_t_kernel(tc, h_attn, Wo, bo, x, gamma, beta, out):
         wo_codes = const.tile([P, PASSES * D_OUT], U32, align_bytes=64)
         wo_scales = const.tile([P, PASSES * D_OUT], U8, align_bytes=64)
         wo_raw_passes = wo_raw[:].rearrange("q (g r) -> q g r", g=PASSES)
-        for g in range(PASSES):
-            nc.sync.dma_start(out=wo_raw_passes[:, g, :], in_=wo_view[:, g, :])
         wo_raw_gct = wo_raw[:].rearrange("q (g t c) -> q g c t", g=PASSES, t=PACK)
         wo_grouped_gct = wo_grouped[:].rearrange("q (g c t) -> q g c t", g=PASSES, t=PACK)
-        for g in range(PASSES):
+
+        def load_wo(g):
+            nc.sync.dma_start(out=wo_raw_passes[:, g, :], in_=wo_view[:, g, :])
+
+        def regroup_wo(g):
             nc.vector.tensor_copy(out=wo_grouped_gct[:, g], in_=wo_raw_gct[:, g])
-        for g in range(PASSES):
+
+        def quantise_wo(g):
             nc.vector.quantize_mx(
                 out=wo_codes[:, g * D_OUT : (g + 1) * D_OUT].bitcast(FP8X4),
                 scales=wo_scales[:, g * D_OUT : (g + 1) * D_OUT],
@@ -113,21 +120,31 @@ def tile_multiheadattn_pb_t_kernel(tc, h_attn, Wo, bo, x, gamma, beta, out):
             half = c % CHUNKS_PER_BATCH
             return slice(half * width, (half + 1) * width)
 
-        def load(c):
+        def load_h(c, tiles):
+            if tiles.start == 0:
+                h_in[c] = h_pool.tile([P, CHUNK_K], BF16, name="h_sb")
+            cols = slice(tiles.start * K_DIM, tiles.stop * K_DIM)
+            chunk = h_view[:, c // CHUNKS_PER_BATCH, chunk_cols(c, CHUNK_K)]
+            nc.sync.dma_start(out=h_in[c][:, cols], in_=chunk[:, cols])
+
+        def load_bias_and_residual(c):
             b = c // CHUNKS_PER_BATCH
-            h_sb = h_pool.tile([P, CHUNK_K], BF16)
-            nc.sync.dma_start(out=h_sb[:], in_=h_view[:, b, chunk_cols(c, CHUNK_K)])
             bo_sb = add_pool.tile([P, CHUNK_D], BF16)
             nc.sync.dma_start(out=bo_sb[:], in_=bo_view[:, b, chunk_cols(c, CHUNK_D)])
             x_sb = add_pool.tile([P, CHUNK_D], BF16)
             nc.sync.dma_start(out=x_sb[:], in_=x_view[:, b, chunk_cols(c, CHUNK_D)])
-            h_in[c], bo_in[c], x_in[c] = h_sb, bo_sb, x_sb
+            bo_in[c], x_in[c] = bo_sb, x_sb
 
-        def transpose(c):
+        def load(c):
+            load_h(c, ALL_TILES)
+            load_bias_and_residual(c)
+
+        def transpose(c, tiles):
+            if tiles.start == 0:
+                h_grouped[c] = grouped_pool.tile([P, CHUNK_K], BF16, align_bytes=64, name="grouped")
             h_words = h_in[c][:].bitcast(F32)
-            grouped = grouped_pool.tile([P, CHUNK_K], BF16, align_bytes=64)
-            grouped_words = grouped[:].bitcast(F32)
-            for j in range(CHUNK_TILES):
+            grouped_words = h_grouped[c][:].bitcast(F32)
+            for j in range(tiles.start, tiles.stop):
                 xt = psum_xt.tile([P, PLANES, P], F32)
                 for a in range(PLANES):
                     g, u = divmod(a, 2)
@@ -139,15 +156,18 @@ def tile_multiheadattn_pb_t_kernel(tc, h_attn, Wo, bo, x, gamma, beta, out):
                     ),
                     in_=xt[:].rearrange("q (g u) r -> q g r u", g=PASSES),
                 )
-            h_grouped[c] = grouped
 
-        def quantise(c):
-            codes = mx_pool.tile([P, CHUNK_TILES * TILE_CODES], U32, align_bytes=64)
-            scales = mx_pool.tile([P, CHUNK_TILES * TILE_CODES], U8, align_bytes=64)
+        def quantise(c, tiles):
+            if tiles.start == 0:
+                width = CHUNK_TILES * TILE_CODES
+                h_codes[c] = mx_pool.tile([P, width], U32, align_bytes=64, name="codes")
+                h_scales[c] = mx_pool.tile([P, width], U8, align_bytes=64, name="scales")
+            words = slice(tiles.start * TILE_CODES, tiles.stop * TILE_CODES)
             nc.vector.quantize_mx(
-                out=codes[:].bitcast(FP8X4), scales=scales[:], in_=h_grouped[c][:]
+                out=h_codes[c][:, words].bitcast(FP8X4),
+                scales=h_scales[c][:, words],
+                in_=h_grouped[c][:, words.start * PACK : words.stop * PACK],
             )
-            h_codes[c], h_scales[c] = codes, scales
 
         def project(c):
             for j in range(CHUNK_TILES):
@@ -166,29 +186,35 @@ def tile_multiheadattn_pb_t_kernel(tc, h_attn, Wo, bo, x, gamma, beta, out):
                     )
                 acc_of[(c, j)] = acc
 
+        def plain_tiles(c):
+            return CHUNK_TILES if c < TENSOR_ADD_FROM else CHUNK_TILES - TENSOR_ADD_TILES
+
         def add_bias_and_residual(c):
+            cols = slice(0, plain_tiles(c) * D_OUT)
+            nc.vector.tensor_tensor(
+                out=o_tiles[c // CHUNKS_PER_BATCH][:, chunk_cols(c, CHUNK_D)][:, cols],
+                in0=bo_in[c][:, cols],
+                in1=x_in[c][:, cols],
+                op=ADD,
+            )
+
+        def tensor_add_bias_and_residual(c):
             o_chunk = o_tiles[c // CHUNKS_PER_BATCH][:, chunk_cols(c, CHUNK_D)]
-            plain_tiles = CHUNK_TILES if c < TENSOR_ADD_FROM else CHUNK_TILES - TENSOR_ADD_TILES
-            if c < GPSIMD_ADD_FROM:
-                nc.vector.tensor_tensor(out=o_chunk, in0=bo_in[c][:], in1=x_in[c][:], op=ADD)
-            else:
-                for j in range(plain_tiles):
-                    cols = slice(j * D_OUT, (j + 1) * D_OUT)
-                    nc.gpsimd.tensor_tensor(
-                        out=o_chunk[:, cols], in0=bo_in[c][:, cols], in1=x_in[c][:, cols], op=ADD
-                    )
-            for j in range(plain_tiles, CHUNK_TILES):
+            for j in range(plain_tiles(c), CHUNK_TILES):
                 cols = slice(j * D_OUT, (j + 1) * D_OUT)
                 bx = psum_plain.tile([P, D_OUT], F32, tag="plain")
                 nc.tensor.matmul(bx[:], lhsT=ident_bf16[:], rhs=bo_in[c][:, cols], start=True, stop=False)
                 nc.tensor.matmul(bx[:], lhsT=ident_bf16[:], rhs=x_in[c][:, cols], start=False, stop=True)
                 nc.scalar.copy(out=o_chunk[:, cols], in_=bx[:])
 
+        def stats_column(c, j):
+            return (c // CHUNKS_PER_BATCH) * STATS + (c % CHUNKS_PER_BATCH) * CHUNK_TILES + j
+
         def add_projection(c):
             o_chunk = o_tiles[c // CHUNKS_PER_BATCH][:, chunk_cols(c, CHUNK_D)]
             for j in range(CHUNK_TILES):
                 o_tile = o_chunk[:, j * D_OUT : (j + 1) * D_OUT]
-                column = c * CHUNK_TILES + j
+                column = stats_column(c, j)
                 nc.vector.scalar_tensor_tensor(
                     out=o_tile,
                     in0=acc_of[(c, j)][:],
@@ -196,94 +222,181 @@ def tile_multiheadattn_pb_t_kernel(tc, h_attn, Wo, bo, x, gamma, beta, out):
                     in1=o_tile,
                     op0=ADD,
                     op1=ADD,
-                    accum_out=tile_sums[:, column : column + 1],
+                    accum_out=stats[:, column : column + 1],
                 )
 
-        def mean(b):
-            columns = slice(b * TILES_PER_BATCH, (b + 1) * TILES_PER_BATCH)
-            totals = psum_plain.tile([P, TILES_PER_BATCH], F32, tag="plain")
-            nc.tensor.matmul(totals[:], lhsT=ones[:], rhs=tile_sums[:, columns], start=True, stop=True)
+        def totals_of(first, width):
+            totals = psum_plain.tile([P, STATS], F32, tag="plain")
+            nc.tensor.matmul(
+                totals[:, :width], lhsT=ones[:], rhs=stats[:, first : first + width], start=True, stop=True
+            )
+            return totals
+
+        def shift(b):
+            first = b * STATS
+            totals = totals_of(first, CHUNK_TILES)
             nc.scalar.activation(
-                out=mean_scratch[:, columns],
-                in_=totals[:],
+                out=scratch[:, first : first + CHUNK_TILES],
+                in_=totals[:, :CHUNK_TILES],
                 func=FUNC.Copy,
-                scale=-1.0 / COUNT,
-                accum_out=neg_mean[:, b : b + 1],
+                scale=-1.0 / (COUNT // CHUNKS_PER_BATCH),
+                accum_out=neg_shift[:, b : b + 1],
             )
 
         def square_tile(c, j):
             b = c // CHUNKS_PER_BATCH
             first = (c % CHUNKS_PER_BATCH) * CHUNK_D + j * D_OUT
-            column = c * CHUNK_TILES + j
+            column = stats_column(c, j) + TILES_PER_BATCH
             squares = scratch_pool.tile([P, D_OUT], BF16)
             nc.scalar.activation(
                 out=squares[:],
                 in_=o_tiles[b][:, first : first + D_OUT],
                 func=FUNC.Square,
-                bias=neg_mean[:, b : b + 1],
-                accum_out=square_sums[:, column : column + 1],
+                bias=neg_shift[:, b : b + 1],
+                accum_out=stats[:, column : column + 1],
             )
 
-        def standard_deviation(b):
-            columns = slice(b * TILES_PER_BATCH, (b + 1) * TILES_PER_BATCH)
-            totals = psum_plain.tile([P, TILES_PER_BATCH], F32, tag="plain")
-            nc.tensor.matmul(totals[:], lhsT=ones[:], rhs=square_sums[:, columns], start=True, stop=True)
+        def moments(b):
+            first = b * STATS
+            middle = first + TILES_PER_BATCH
+            totals = totals_of(first, STATS)
             nc.scalar.activation(
-                out=var_scratch[:, columns],
-                in_=totals[:],
+                out=scratch[:, first:middle],
+                in_=totals[:, :TILES_PER_BATCH],
                 func=FUNC.Copy,
-                scale=1.0 / COUNT,
-                accum_out=var[:, b : b + 1],
+                scale=-1.0 / COUNT,
+                accum_out=neg_mean[:, b : b + 1],
             )
-            nc.scalar.activation(out=std[:, b : b + 1], in_=var[:, b : b + 1], func=FUNC.Sqrt, bias=eps[:])
+            nc.scalar.activation(
+                out=scratch[:, middle : first + STATS],
+                in_=totals[:, TILES_PER_BATCH:],
+                func=FUNC.Identity,
+                scale=1.0 / COUNT,
+                bias=eps_part[:],
+                accum_out=mean_square[:, b : b + 1],
+            )
+            nc.scalar.activation(
+                out=gap_square[:, b : b + 1],
+                in_=neg_mean[:, b : b + 1],
+                func=FUNC.Square,
+                scale=-1.0,
+                bias=neg_shift[:, b : b + 1],
+            )
+            nc.scalar.activation(
+                out=std[:, b : b + 1],
+                in_=gap_square[:, b : b + 1],
+                func=FUNC.Sqrt,
+                scale=-1.0,
+                bias=mean_square[:, b : b + 1],
+            )
 
-        def normalise_and_store(c):
-            b = c // CHUNKS_PER_BATCH
-            if c % CHUNKS_PER_BATCH == 0:
-                nc.vector.reciprocal(out=rstd[:, b : b + 1], in_=std[:, b : b + 1])
-            first = (c % CHUNKS_PER_BATCH) * CHUNK_D
-            pieces = [slice(first + n * PIECE_D, first + (n + 1) * PIECE_D) for n in range(NORM_PIECES)]
-            for piece in pieces:
-                nc.vector.scalar_tensor_tensor(
-                    out=o_tiles[b][:, piece],
-                    in0=o_tiles[b][:, piece],
-                    scalar=neg_mean[:, b : b + 1],
-                    in1=gamma_sb[:, piece],
-                    op0=ADD,
-                    op1=MULT,
-                )
-            for piece in pieces:
-                nc.vector.scalar_tensor_tensor(
-                    out=o_tiles[b][:, piece],
-                    in0=o_tiles[b][:, piece],
-                    scalar=rstd[:, b : b + 1],
-                    in1=beta_sb[:, piece],
-                    op0=MULT,
-                    op1=ADD,
-                )
-                nc.sync.dma_start(out=out_view[:, b, piece], in_=o_tiles[b][:, piece])
+        def reciprocal(b):
+            nc.vector.reciprocal(out=rstd[:, b : b + 1], in_=std[:, b : b + 1])
+
+        def piece_cols(p):
+            b, n = divmod(p, PIECES)
+            return b, slice(n * PIECE_D, (n + 1) * PIECE_D)
+
+        def subtract_mean_and_scale(p):
+            b, cols = piece_cols(p)
+            nc.vector.scalar_tensor_tensor(
+                out=o_tiles[b][:, cols],
+                in0=o_tiles[b][:, cols],
+                scalar=neg_mean[:, b : b + 1],
+                in1=gamma_sb[:, cols],
+                op0=ADD,
+                op1=MULT,
+            )
+
+        def normalise_and_store(p):
+            b, cols = piece_cols(p)
+            nc.vector.scalar_tensor_tensor(
+                out=o_tiles[b][:, cols],
+                in0=o_tiles[b][:, cols],
+                scalar=rstd[:, b : b + 1],
+                in1=beta_sb[:, cols],
+                op0=MULT,
+                op1=ADD,
+            )
+            nc.sync.dma_start(out=out_view[:, b, cols], in_=o_tiles[b][:, cols])
+
+        def normalise(pieces):
+            for p in pieces:
+                subtract_mean_and_scale(p)
+            for p in pieces:
+                if p % PIECES == 0:
+                    reciprocal(p // PIECES)
+                normalise_and_store(p)
 
         def is_chunk(c):
             return 0 <= c < CHUNKS
 
-        for c in range(INPUT_BUFS):
-            load(c)
-        nc.sync.dma_start(out=gamma_sb[:], in_=gamma_view)
-        nc.sync.dma_start(out=beta_sb[:], in_=beta_view)
-        for c in range(CHUNKS):
-            transpose(c)
-            quantise(c)
-            add_bias_and_residual(c)
-            project(c)
-            add_projection(c)
-            if is_chunk(c + INPUT_BUFS):
-                load(c + INPUT_BUFS)
-            if c % CHUNKS_PER_BATCH == CHUNKS_PER_BATCH - 1:
-                b = c // CHUNKS_PER_BATCH
-                mean(b)
-                for cc in range(c - CHUNKS_PER_BATCH + 1, c + 1):
-                    for j in range(CHUNK_TILES):
-                        square_tile(cc, j)
-                standard_deviation(b)
-        for c in range(CHUNKS):
-            normalise_and_store(c)
+        def squares(i):
+            for j in range(CHUNK_TILES):
+                square_tile(i, j)
+
+        def first_step(i):
+            if is_chunk(i + INPUT_BUFS):
+                load(i + INPUT_BUFS)
+            add_projection(i)
+            if i % CHUNKS_PER_BATCH == 0:
+                shift(i // CHUNKS_PER_BATCH)
+            transpose(i + 2, ALL_TILES)
+            quantise(i + 1, ALL_TILES)
+            project(i + 1)
+            add_bias_and_residual(i + 1)
+            squares(i)
+            if i % CHUNKS_PER_BATCH == CHUNKS_PER_BATCH - 1:
+                moments(i // CHUNKS_PER_BATCH)
+
+        def step(i):
+            if is_chunk(i + INPUT_BUFS):
+                load(i + INPUT_BUFS)
+            if is_chunk(i + 2):
+                transpose(i + 2, FIRST_HALF)
+            if is_chunk(i + 1):
+                quantise(i + 1, ALL_TILES)
+            add_projection(i)
+            if is_chunk(i + 1):
+                project(i + 1)
+            if i % CHUNKS_PER_BATCH == 0:
+                shift(i // CHUNKS_PER_BATCH)
+            squares(i)
+            if i % CHUNKS_PER_BATCH == CHUNKS_PER_BATCH - 1:
+                moments(i // CHUNKS_PER_BATCH)
+            if is_chunk(i + 2):
+                transpose(i + 2, SECOND_HALF)
+                tensor_add_bias_and_residual(i + 2)
+            normalise([PIECES_PER_STEP * (i - CHUNKS_PER_BATCH) + n for n in range(PIECES_PER_STEP)])
+            if is_chunk(i + 1):
+                add_bias_and_residual(i + 1)
+
+        with tc.manual_schedule():
+            load_h(0, FIRST_HALF)
+            for g in range(PASSES):
+                load_wo(g)
+            load_h(0, SECOND_HALF)
+            load_bias_and_residual(0)
+            load(1)
+            load(2)
+            load_h(3, ALL_TILES)
+            nc.sync.dma_start(out=gamma_sb[:], in_=gamma_view)
+            nc.sync.dma_start(out=beta_sb[:], in_=beta_view)
+            load_bias_and_residual(3)
+            load(4)
+            transpose(0, FIRST_HALF)
+            regroup_wo(0)
+            quantise(0, FIRST_HALF)
+            regroup_wo(1)
+            transpose(0, SECOND_HALF)
+            for g in range(PASSES):
+                quantise_wo(g)
+            quantise(0, SECOND_HALF)
+            project(0)
+            transpose(1, ALL_TILES)
+            add_bias_and_residual(0)
+            for i in range(CHUNKS_PER_BATCH):
+                first_step(i)
+            for i in range(CHUNKS_PER_BATCH, CHUNKS):
+                step(i)
+            normalise(range(PIECES * (BATCH - 1), PIECES * BATCH))

@@ -37,8 +37,8 @@ COUNT = SEQ * D_OUT
 INPUT_BUFS = 5
 STAGE_BUFS = 3
 
-TENSOR_ADD_FROM = CHUNKS // 2
-TENSOR_ADD_TILES = 3
+OTHERS_ADD_FROM = CHUNKS_PER_BATCH
+GPSIMD_ADD_TILES = 2
 ALL_TILES = slice(0, CHUNK_TILES)
 FIRST_HALF = slice(0, HALF_TILES)
 SECOND_HALF = slice(HALF_TILES, CHUNK_TILES)
@@ -64,6 +64,7 @@ def tile_multiheadattn_pb_t_kernel(tc, h_attn, Wo, bo, x, gamma, beta, out):
         grouped_pool = ctx.enter_context(tc.tile_pool(name="grouped_pool", bufs=STAGE_BUFS))
         mx_pool = ctx.enter_context(tc.tile_pool(name="mx_pool", bufs=STAGE_BUFS))
         scratch_pool = ctx.enter_context(tc.tile_pool(name="scratch_pool", bufs=4))
+        gpsimd_pool = ctx.enter_context(tc.tile_pool(name="gpsimd_pool", bufs=1))
         psum_xt = ctx.enter_context(tc.psum_pool(name="psum_xt", bufs=2))
         psum_acc = ctx.enter_context(tc.psum_pool(name="psum_acc", bufs=CHUNK_TILES))
         psum_plain = ctx.enter_context(tc.psum_pool(name="psum_plain", bufs=2))
@@ -114,7 +115,7 @@ def tile_multiheadattn_pb_t_kernel(tc, h_attn, Wo, bo, x, gamma, beta, out):
 
         h_in, bo_in, x_in = {}, {}, {}
         h_grouped, h_codes, h_scales = {}, {}, {}
-        acc_of = {}
+        acc_of, gpsimd_sum_of = {}, {}
 
         def chunk_cols(c, width):
             half = c % CHUNKS_PER_BATCH
@@ -186,21 +187,26 @@ def tile_multiheadattn_pb_t_kernel(tc, h_attn, Wo, bo, x, gamma, beta, out):
                     )
                 acc_of[(c, j)] = acc
 
-        def plain_tiles(c):
-            return CHUNK_TILES if c < TENSOR_ADD_FROM else CHUNK_TILES - TENSOR_ADD_TILES
-
         def add_bias_and_residual(c):
-            cols = slice(0, plain_tiles(c) * D_OUT)
-            nc.vector.tensor_tensor(
-                out=o_tiles[c // CHUNKS_PER_BATCH][:, chunk_cols(c, CHUNK_D)][:, cols],
-                in0=bo_in[c][:, cols],
-                in1=x_in[c][:, cols],
-                op=ADD,
-            )
+            if c < OTHERS_ADD_FROM:
+                nc.vector.tensor_tensor(
+                    out=o_tiles[c // CHUNKS_PER_BATCH][:, chunk_cols(c, CHUNK_D)],
+                    in0=bo_in[c][:],
+                    in1=x_in[c][:],
+                    op=ADD,
+                )
+                return
+            for j in range(GPSIMD_ADD_TILES):
+                cols = slice(j * D_OUT, (j + 1) * D_OUT)
+                bx = gpsimd_pool.tile([P, D_OUT], F32, name="bx%d" % j)
+                nc.gpsimd.tensor_tensor(out=bx[:], in0=bo_in[c][:, cols], in1=x_in[c][:, cols], op=ADD)
+                gpsimd_sum_of[(c, j)] = bx
 
         def tensor_add_bias_and_residual(c):
+            if c < OTHERS_ADD_FROM:
+                return
             o_chunk = o_tiles[c // CHUNKS_PER_BATCH][:, chunk_cols(c, CHUNK_D)]
-            for j in range(plain_tiles(c), CHUNK_TILES):
+            for j in range(GPSIMD_ADD_TILES, CHUNK_TILES):
                 cols = slice(j * D_OUT, (j + 1) * D_OUT)
                 bx = psum_plain.tile([P, D_OUT], F32, tag="plain")
                 nc.tensor.matmul(bx[:], lhsT=ident_bf16[:], rhs=bo_in[c][:, cols], start=True, stop=False)
@@ -214,12 +220,13 @@ def tile_multiheadattn_pb_t_kernel(tc, h_attn, Wo, bo, x, gamma, beta, out):
             o_chunk = o_tiles[c // CHUNKS_PER_BATCH][:, chunk_cols(c, CHUNK_D)]
             for j in range(CHUNK_TILES):
                 o_tile = o_chunk[:, j * D_OUT : (j + 1) * D_OUT]
+                gpsimd_sum = gpsimd_sum_of.get((c, j))
                 column = stats_column(c, j)
                 nc.vector.scalar_tensor_tensor(
                     out=o_tile,
                     in0=acc_of[(c, j)][:],
                     scalar=0.0,
-                    in1=o_tile,
+                    in1=o_tile if gpsimd_sum is None else gpsimd_sum[:],
                     op0=ADD,
                     op1=ADD,
                     accum_out=stats[:, column : column + 1],
@@ -345,6 +352,7 @@ def tile_multiheadattn_pb_t_kernel(tc, h_attn, Wo, bo, x, gamma, beta, out):
             quantise(i + 1, ALL_TILES)
             project(i + 1)
             add_bias_and_residual(i + 1)
+            tensor_add_bias_and_residual(i + 2)
             squares(i)
             if i % CHUNKS_PER_BATCH == CHUNKS_PER_BATCH - 1:
                 moments(i // CHUNKS_PER_BATCH)
@@ -353,7 +361,7 @@ def tile_multiheadattn_pb_t_kernel(tc, h_attn, Wo, bo, x, gamma, beta, out):
             if is_chunk(i + INPUT_BUFS):
                 load(i + INPUT_BUFS)
             if is_chunk(i + 2):
-                transpose(i + 2, FIRST_HALF)
+                transpose(i + 2, ALL_TILES)
             if is_chunk(i + 1):
                 quantise(i + 1, ALL_TILES)
             add_projection(i)
@@ -362,11 +370,10 @@ def tile_multiheadattn_pb_t_kernel(tc, h_attn, Wo, bo, x, gamma, beta, out):
             if i % CHUNKS_PER_BATCH == 0:
                 shift(i // CHUNKS_PER_BATCH)
             squares(i)
+            if is_chunk(i + 2):
+                tensor_add_bias_and_residual(i + 2)
             if i % CHUNKS_PER_BATCH == CHUNKS_PER_BATCH - 1:
                 moments(i // CHUNKS_PER_BATCH)
-            if is_chunk(i + 2):
-                transpose(i + 2, SECOND_HALF)
-                tensor_add_bias_and_residual(i + 2)
             normalise([PIECES_PER_STEP * (i - CHUNKS_PER_BATCH) + n for n in range(PIECES_PER_STEP)])
             if is_chunk(i + 1):
                 add_bias_and_residual(i + 1)

@@ -37,7 +37,7 @@ COUNT = SEQ * D_OUT
 INPUT_BUFS = 5
 STAGE_BUFS = 3
 
-OTHERS_ADD_FROM = CHUNKS_PER_BATCH
+OTHERS_ADD_FROM = 3
 GPSIMD_ADD_TILES = 2
 ALL_TILES = slice(0, CHUNK_TILES)
 FIRST_HALF = slice(0, HALF_TILES)
@@ -170,8 +170,8 @@ def tile_multiheadattn_pb_t_kernel(tc, h_attn, Wo, bo, x, gamma, beta, out):
                 in_=h_grouped[c][:, words.start * PACK : words.stop * PACK],
             )
 
-        def project(c):
-            for j in range(CHUNK_TILES):
+        def project(c, tiles):
+            for j in range(tiles.start, tiles.stop):
                 acc = psum_acc.tile([P, D_OUT], F32)
                 for g in range(PASSES):
                     tokens = slice((j * PASSES + g) * P, (j * PASSES + g + 1) * P)
@@ -241,13 +241,9 @@ def tile_multiheadattn_pb_t_kernel(tc, h_attn, Wo, bo, x, gamma, beta, out):
 
         def shift(b):
             first = b * STATS
-            totals = totals_of(first, CHUNK_TILES)
+            totals = totals_of(first, 1)
             nc.scalar.activation(
-                out=scratch[:, first : first + CHUNK_TILES],
-                in_=totals[:, :CHUNK_TILES],
-                func=FUNC.Copy,
-                scale=-1.0 / (COUNT // CHUNKS_PER_BATCH),
-                accum_out=neg_shift[:, b : b + 1],
+                out=neg_shift[:, b : b + 1], in_=totals[:, :1], func=FUNC.Copy, scale=-1.0 / (P * D_OUT)
             )
 
         def square_tile(c, j):
@@ -342,21 +338,6 @@ def tile_multiheadattn_pb_t_kernel(tc, h_attn, Wo, bo, x, gamma, beta, out):
             for j in range(CHUNK_TILES):
                 square_tile(i, j)
 
-        def first_step(i):
-            if is_chunk(i + INPUT_BUFS):
-                load(i + INPUT_BUFS)
-            add_projection(i)
-            if i % CHUNKS_PER_BATCH == 0:
-                shift(i // CHUNKS_PER_BATCH)
-            transpose(i + 2, ALL_TILES)
-            quantise(i + 1, ALL_TILES)
-            project(i + 1)
-            add_bias_and_residual(i + 1)
-            tensor_add_bias_and_residual(i + 2)
-            squares(i)
-            if i % CHUNKS_PER_BATCH == CHUNKS_PER_BATCH - 1:
-                moments(i // CHUNKS_PER_BATCH)
-
         def step(i):
             if is_chunk(i + INPUT_BUFS):
                 load(i + INPUT_BUFS)
@@ -365,10 +346,10 @@ def tile_multiheadattn_pb_t_kernel(tc, h_attn, Wo, bo, x, gamma, beta, out):
             if is_chunk(i + 1):
                 quantise(i + 1, ALL_TILES)
             add_projection(i)
-            if is_chunk(i + 1):
-                project(i + 1)
             if i % CHUNKS_PER_BATCH == 0:
                 shift(i // CHUNKS_PER_BATCH)
+            if is_chunk(i + 1):
+                project(i + 1, ALL_TILES)
             squares(i)
             if is_chunk(i + 2):
                 tensor_add_bias_and_residual(i + 2)
@@ -395,15 +376,31 @@ def tile_multiheadattn_pb_t_kernel(tc, h_attn, Wo, bo, x, gamma, beta, out):
             regroup_wo(0)
             quantise(0, FIRST_HALF)
             regroup_wo(1)
-            transpose(0, SECOND_HALF)
             for g in range(PASSES):
                 quantise_wo(g)
+            transpose(0, SECOND_HALF)
             quantise(0, SECOND_HALF)
-            project(0)
-            transpose(1, ALL_TILES)
             add_bias_and_residual(0)
-            for i in range(CHUNKS_PER_BATCH):
-                first_step(i)
+            project(0, ALL_TILES)
+            transpose(1, ALL_TILES)
+            add_projection(0)
+            shift(0)
+            quantise(1, ALL_TILES)
+            add_bias_and_residual(1)
+            for j in range(CHUNK_TILES):
+                transpose(2, slice(j, j + 1))
+                project(1, slice(j, j + 1))
+                square_tile(0, j)
+            load(5)
+            add_bias_and_residual(2)
+            add_projection(1)
+            quantise(2, ALL_TILES)
+            transpose(3, ALL_TILES)
+            project(2, ALL_TILES)
+            squares(1)
+            moments(0)
+            tensor_add_bias_and_residual(3)
+            load(6)
             for i in range(CHUNKS_PER_BATCH, CHUNKS):
                 step(i)
             normalise(range(PIECES * (BATCH - 1), PIECES * BATCH))

@@ -64,7 +64,7 @@ def tile_multiheadattn_pb_t_kernel(tc, h_attn, Wo, bo, x, gamma, beta, out):
         grouped_pool = ctx.enter_context(tc.tile_pool(name="grouped_pool", bufs=STAGE_BUFS))
         mx_pool = ctx.enter_context(tc.tile_pool(name="mx_pool", bufs=STAGE_BUFS))
         scratch_pool = ctx.enter_context(tc.tile_pool(name="scratch_pool", bufs=4))
-        gpsimd_pool = ctx.enter_context(tc.tile_pool(name="gpsimd_pool", bufs=1))
+        gpsimd_pool = ctx.enter_context(tc.tile_pool(name="gpsimd_pool", bufs=2))
         psum_xt = ctx.enter_context(tc.psum_pool(name="psum_xt", bufs=2))
         psum_acc = ctx.enter_context(tc.psum_pool(name="psum_acc", bufs=CHUNK_TILES))
         psum_plain = ctx.enter_context(tc.psum_pool(name="psum_plain", bufs=2))
@@ -196,9 +196,10 @@ def tile_multiheadattn_pb_t_kernel(tc, h_attn, Wo, bo, x, gamma, beta, out):
                     op=ADD,
                 )
                 return
-            for j in range(GPSIMD_ADD_TILES):
+            sums = [gpsimd_pool.tile([P, D_OUT], F32, name="bx%d" % j) for j in range(GPSIMD_ADD_TILES)]
+            nc.vector.memset(sums[0][:, :1], 0.0)
+            for j, bx in enumerate(sums):
                 cols = slice(j * D_OUT, (j + 1) * D_OUT)
-                bx = gpsimd_pool.tile([P, D_OUT], F32, name="bx%d" % j)
                 nc.gpsimd.tensor_tensor(out=bx[:], in0=bo_in[c][:, cols], in1=x_in[c][:, cols], op=ADD)
                 gpsimd_sum_of[(c, j)] = bx
 
@@ -345,6 +346,7 @@ def tile_multiheadattn_pb_t_kernel(tc, h_attn, Wo, bo, x, gamma, beta, out):
                 transpose(i + 2, ALL_TILES)
             if is_chunk(i + 1):
                 quantise(i + 1, ALL_TILES)
+                add_bias_and_residual(i + 1)
             add_projection(i)
             if i % CHUNKS_PER_BATCH == 0:
                 shift(i // CHUNKS_PER_BATCH)
@@ -356,8 +358,6 @@ def tile_multiheadattn_pb_t_kernel(tc, h_attn, Wo, bo, x, gamma, beta, out):
             if i % CHUNKS_PER_BATCH == CHUNKS_PER_BATCH - 1:
                 moments(i // CHUNKS_PER_BATCH)
             normalise([PIECES_PER_STEP * (i - CHUNKS_PER_BATCH) + n for n in range(PIECES_PER_STEP)])
-            if is_chunk(i + 1):
-                add_bias_and_residual(i + 1)
 
         with tc.manual_schedule():
             load_h(0, FIRST_HALF)

@@ -29,9 +29,6 @@ WORDS = K_DIM // 2
 PLANES = WORDS // P
 TILE_CODES = K_DIM // PACK
 HALF_TILES = CHUNK_TILES // 2
-PIECES = 4
-PIECE_D = BATCH_D // PIECES
-PIECES_PER_STEP = PIECES // CHUNKS_PER_BATCH
 COUNT = SEQ * D_OUT
 
 INPUT_BUFS = 5
@@ -196,12 +193,11 @@ def tile_multiheadattn_pb_t_kernel(tc, h_attn, Wo, bo, x, gamma, beta, out):
                     op=ADD,
                 )
                 return
-            sums = [gpsimd_pool.tile([P, D_OUT], F32, name="bx%d" % j) for j in range(GPSIMD_ADD_TILES)]
-            nc.vector.memset(sums[0][:, :1], 0.0)
-            for j, bx in enumerate(sums):
-                cols = slice(j * D_OUT, (j + 1) * D_OUT)
-                nc.gpsimd.tensor_tensor(out=bx[:], in0=bo_in[c][:, cols], in1=x_in[c][:, cols], op=ADD)
-                gpsimd_sum_of[(c, j)] = bx
+            cols = slice(0, GPSIMD_ADD_TILES * D_OUT)
+            bx = gpsimd_pool.tile([P, GPSIMD_ADD_TILES * D_OUT], F32)
+            nc.vector.memset(bx[:, :1], 0.0)
+            nc.gpsimd.tensor_tensor(out=bx[:], in0=bo_in[c][:, cols], in1=x_in[c][:, cols], op=ADD)
+            gpsimd_sum_of[c] = bx
 
         def tensor_add_bias_and_residual(c):
             if c < OTHERS_ADD_FROM:
@@ -220,14 +216,15 @@ def tile_multiheadattn_pb_t_kernel(tc, h_attn, Wo, bo, x, gamma, beta, out):
         def add_projection(c):
             o_chunk = o_tiles[c // CHUNKS_PER_BATCH][:, chunk_cols(c, CHUNK_D)]
             for j in range(CHUNK_TILES):
-                o_tile = o_chunk[:, j * D_OUT : (j + 1) * D_OUT]
-                gpsimd_sum = gpsimd_sum_of.get((c, j))
+                cols = slice(j * D_OUT, (j + 1) * D_OUT)
+                o_tile = o_chunk[:, cols]
+                in_gpsimd_sum = c in gpsimd_sum_of and j < GPSIMD_ADD_TILES
                 column = stats_column(c, j)
                 nc.vector.scalar_tensor_tensor(
                     out=o_tile,
                     in0=acc_of[(c, j)][:],
                     scalar=0.0,
-                    in1=o_tile if gpsimd_sum is None else gpsimd_sum[:],
+                    in1=gpsimd_sum_of[c][:, cols] if in_gpsimd_sum else o_tile,
                     op0=ADD,
                     op1=ADD,
                     accum_out=stats[:, column : column + 1],
@@ -297,40 +294,24 @@ def tile_multiheadattn_pb_t_kernel(tc, h_attn, Wo, bo, x, gamma, beta, out):
         def reciprocal(b):
             nc.vector.reciprocal(out=rstd[:, b : b + 1], in_=std[:, b : b + 1])
 
-        def piece_cols(p):
-            b, n = divmod(p, PIECES)
-            return b, slice(n * PIECE_D, (n + 1) * PIECE_D)
+        def part_of(c, part):
+            b = c // CHUNKS_PER_BATCH
+            first = (c % CHUNKS_PER_BATCH) * CHUNK_D
+            cols = slice(first + part.start, first + part.stop)
+            return b, o_tiles[b][:, cols], cols
 
-        def subtract_mean_and_scale(p):
-            b, cols = piece_cols(p)
+        def subtract_mean_and_scale(c, part):
+            b, o, cols = part_of(c, part)
             nc.vector.scalar_tensor_tensor(
-                out=o_tiles[b][:, cols],
-                in0=o_tiles[b][:, cols],
-                scalar=neg_mean[:, b : b + 1],
-                in1=gamma_sb[:, cols],
-                op0=ADD,
-                op1=MULT,
+                out=o, in0=o, scalar=neg_mean[:, b : b + 1], in1=gamma_sb[:, cols], op0=ADD, op1=MULT
             )
 
-        def normalise_and_store(p):
-            b, cols = piece_cols(p)
+        def normalise_and_store(c, part):
+            b, o, cols = part_of(c, part)
             nc.vector.scalar_tensor_tensor(
-                out=o_tiles[b][:, cols],
-                in0=o_tiles[b][:, cols],
-                scalar=rstd[:, b : b + 1],
-                in1=beta_sb[:, cols],
-                op0=MULT,
-                op1=ADD,
+                out=o, in0=o, scalar=rstd[:, b : b + 1], in1=beta_sb[:, cols], op0=MULT, op1=ADD
             )
-            nc.sync.dma_start(out=out_view[:, b, cols], in_=o_tiles[b][:, cols])
-
-        def normalise(pieces):
-            for p in pieces:
-                subtract_mean_and_scale(p)
-            for p in pieces:
-                if p % PIECES == 0:
-                    reciprocal(p // PIECES)
-                normalise_and_store(p)
+            nc.sync.dma_start(out=out_view[:, b, cols], in_=o)
 
         def is_chunk(c):
             return 0 <= c < CHUNKS
@@ -339,25 +320,35 @@ def tile_multiheadattn_pb_t_kernel(tc, h_attn, Wo, bo, x, gamma, beta, out):
             for j in range(CHUNK_TILES):
                 square_tile(i, j)
 
+        whole = slice(0, CHUNK_D)
+
         def step(i):
+            done = i - CHUNKS_PER_BATCH
             if is_chunk(i + INPUT_BUFS):
                 load(i + INPUT_BUFS)
             if is_chunk(i + 2):
                 transpose(i + 2, ALL_TILES)
             if is_chunk(i + 1):
                 quantise(i + 1, ALL_TILES)
+            if done > 0:
+                subtract_mean_and_scale(done, whole)
+            if is_chunk(i + 1):
                 add_bias_and_residual(i + 1)
             add_projection(i)
+            if done == 0:
+                subtract_mean_and_scale(done, whole)
+            if done % CHUNKS_PER_BATCH == 0:
+                reciprocal(done // CHUNKS_PER_BATCH)
+            normalise_and_store(done, whole)
             if i % CHUNKS_PER_BATCH == 0:
                 shift(i // CHUNKS_PER_BATCH)
             if is_chunk(i + 1):
                 project(i + 1, ALL_TILES)
             squares(i)
-            if is_chunk(i + 2):
-                tensor_add_bias_and_residual(i + 2)
             if i % CHUNKS_PER_BATCH == CHUNKS_PER_BATCH - 1:
                 moments(i // CHUNKS_PER_BATCH)
-            normalise([PIECES_PER_STEP * (i - CHUNKS_PER_BATCH) + n for n in range(PIECES_PER_STEP)])
+            if is_chunk(i + 2):
+                tensor_add_bias_and_residual(i + 2)
 
         with tc.manual_schedule():
             load_h(0, FIRST_HALF)
@@ -403,4 +394,12 @@ def tile_multiheadattn_pb_t_kernel(tc, h_attn, Wo, bo, x, gamma, beta, out):
             load(6)
             for i in range(CHUNKS_PER_BATCH, CHUNKS):
                 step(i)
-            normalise(range(PIECES * (BATCH - 1), PIECES * BATCH))
+            reciprocal(BATCH - 1)
+            quarter = CHUNK_D // 4
+            for c, width in ((CHUNKS - 2, 2 * quarter), (CHUNKS - 1, quarter)):
+                for first in range(0, CHUNK_D, 2 * width):
+                    pieces = [slice(first + n * width, first + (n + 1) * width) for n in range(2)]
+                    for piece in pieces:
+                        subtract_mean_and_scale(c, piece)
+                    for piece in pieces:
+                        normalise_and_store(c, piece)

@@ -36,6 +36,7 @@ STAGE_BUFS = 3
 
 OTHERS_ADD_FROM = 3
 GPSIMD_ADD_TILES = 2
+TENSOR_NORM_TILES = 2
 ALL_TILES = slice(0, CHUNK_TILES)
 FIRST_HALF = slice(0, HALF_TILES)
 SECOND_HALF = slice(HALF_TILES, CHUNK_TILES)
@@ -88,20 +89,21 @@ def tile_multiheadattn_pb_t_kernel(tc, h_attn, Wo, bo, x, gamma, beta, out):
         o_tiles = [const.tile([P, BATCH_D], F32, name="o%d" % b) for b in range(BATCH)]
         gamma_sb = const.tile([P, BATCH_D], BF16)
         beta_sb = const.tile([P, BATCH_D], BF16)
+        diagonal = const.tile([P, P], F32)
 
         wo_raw = const.tile([P, PASSES * PACK * D_OUT], BF16)
         wo_grouped = const.tile([P, PASSES * D_OUT * PACK], BF16, align_bytes=64)
         wo_codes = const.tile([P, PASSES * D_OUT], U32, align_bytes=64)
         wo_scales = const.tile([P, PASSES * D_OUT], U8, align_bytes=64)
         wo_raw_passes = wo_raw[:].rearrange("q (g r) -> q g r", g=PASSES)
-        wo_raw_gct = wo_raw[:].rearrange("q (g t c) -> q g c t", g=PASSES, t=PACK)
-        wo_grouped_gct = wo_grouped[:].rearrange("q (g c t) -> q g c t", g=PASSES, t=PACK)
+        wo_raw_cti = wo_raw[:].rearrange("q (g t c i) -> q g c t i", g=PASSES, t=PACK, i=4)
+        wo_grouped_cti = wo_grouped[:].rearrange("q (g c i t) -> q g c t i", g=PASSES, i=4, t=PACK)
 
         def load_wo(g):
             nc.sync.dma_start(out=wo_raw_passes[:, g, :], in_=wo_view[:, g, :])
 
         def regroup_wo(g):
-            nc.vector.tensor_copy(out=wo_grouped_gct[:, g], in_=wo_raw_gct[:, g])
+            nc.vector.tensor_copy(out=wo_grouped_cti[:, g], in_=wo_raw_cti[:, g])
 
         def quantise_wo(g):
             nc.vector.quantize_mx(
@@ -193,10 +195,11 @@ def tile_multiheadattn_pb_t_kernel(tc, h_attn, Wo, bo, x, gamma, beta, out):
                     op=ADD,
                 )
                 return
-            cols = slice(0, GPSIMD_ADD_TILES * D_OUT)
             bx = gpsimd_pool.tile([P, GPSIMD_ADD_TILES * D_OUT], F32)
+            rest = slice(896, GPSIMD_ADD_TILES * D_OUT)
+            nc.vector.tensor_tensor(out=bx[:, rest], in0=bo_in[c][:, rest], in1=x_in[c][:, rest], op=ADD)
             nc.vector.memset(bx[:, :1], 0.0)
-            nc.gpsimd.tensor_tensor(out=bx[:], in0=bo_in[c][:, cols], in1=x_in[c][:, cols], op=ADD)
+            nc.gpsimd.tensor_tensor(out=bx[:, :896], in0=bo_in[c][:, :896], in1=x_in[c][:, :896], op=ADD)
             gpsimd_sum_of[c] = bx
 
         def tensor_add_bias_and_residual(c):
@@ -321,6 +324,7 @@ def tile_multiheadattn_pb_t_kernel(tc, h_attn, Wo, bo, x, gamma, beta, out):
                 square_tile(i, j)
 
         whole = slice(0, CHUNK_D)
+        halves = [slice(0, CHUNK_D // 2), slice(CHUNK_D // 2, CHUNK_D)]
 
         def step(i):
             done = i - CHUNKS_PER_BATCH
@@ -329,17 +333,20 @@ def tile_multiheadattn_pb_t_kernel(tc, h_attn, Wo, bo, x, gamma, beta, out):
             if is_chunk(i + 2):
                 transpose(i + 2, ALL_TILES)
             if is_chunk(i + 1):
-                quantise(i + 1, ALL_TILES)
-            if done > 0:
+                for half in (FIRST_HALF, SECOND_HALF) if done == 0 else (ALL_TILES,):
+                    quantise(i + 1, half)
+            new_statistics = done % CHUNKS_PER_BATCH == 0
+            if not new_statistics:
                 subtract_mean_and_scale(done, whole)
             if is_chunk(i + 1):
                 add_bias_and_residual(i + 1)
             add_projection(i)
-            if done == 0:
-                subtract_mean_and_scale(done, whole)
-            if done % CHUNKS_PER_BATCH == 0:
+            if new_statistics:
+                for half in halves:
+                    subtract_mean_and_scale(done, half)
                 reciprocal(done // CHUNKS_PER_BATCH)
-            normalise_and_store(done, whole)
+            for part in halves if new_statistics else [whole]:
+                normalise_and_store(done, part)
             if i % CHUNKS_PER_BATCH == 0:
                 shift(i // CHUNKS_PER_BATCH)
             if is_chunk(i + 1):
@@ -376,7 +383,8 @@ def tile_multiheadattn_pb_t_kernel(tc, h_attn, Wo, bo, x, gamma, beta, out):
             transpose(1, ALL_TILES)
             add_projection(0)
             shift(0)
-            quantise(1, ALL_TILES)
+            for half in (FIRST_HALF, SECOND_HALF):
+                quantise(1, half)
             add_bias_and_residual(1)
             for j in range(CHUNK_TILES):
                 transpose(2, slice(j, j + 1))
@@ -385,7 +393,8 @@ def tile_multiheadattn_pb_t_kernel(tc, h_attn, Wo, bo, x, gamma, beta, out):
             load(5)
             add_bias_and_residual(2)
             add_projection(1)
-            quantise(2, ALL_TILES)
+            for half in (FIRST_HALF, SECOND_HALF):
+                quantise(2, half)
             transpose(3, ALL_TILES)
             project(2, ALL_TILES)
             squares(1)
@@ -394,12 +403,25 @@ def tile_multiheadattn_pb_t_kernel(tc, h_attn, Wo, bo, x, gamma, beta, out):
             load(6)
             for i in range(CHUNKS_PER_BATCH, CHUNKS):
                 step(i)
-            reciprocal(BATCH - 1)
-            quarter = CHUNK_D // 4
-            for c, width in ((CHUNKS - 2, 2 * quarter), (CHUNKS - 1, quarter)):
-                for first in range(0, CHUNK_D, 2 * width):
-                    pieces = [slice(first + n * width, first + (n + 1) * width) for n in range(2)]
-                    for piece in pieces:
-                        subtract_mean_and_scale(c, piece)
-                    for piece in pieces:
-                        normalise_and_store(c, piece)
+            b, c = BATCH - 1, CHUNKS - 1
+            tiles = [slice(j * D_OUT, (j + 1) * D_OUT) for j in range(CHUNK_TILES)]
+            shared = tiles[CHUNK_TILES - TENSOR_NORM_TILES :]
+            own = [(c - 1, tile) for tile in tiles] + [(c, tile) for tile in tiles if tile not in shared]
+            reciprocal(b)
+            nc.scalar.activation(out=diagonal[:], in_=ident[:], func=FUNC.Copy, scale=rstd[:, b : b + 1])
+            for tile in shared:
+                subtract_mean_and_scale(c, tile)
+            for tile in shared:
+                o, cols = part_of(c, tile)[1:]
+                total = psum_plain.tile([P, D_OUT], F32, tag="plain")
+                nc.tensor.matmul(total[:], lhsT=diagonal[:], rhs=o, start=True, stop=False)
+                nc.tensor.matmul(total[:], lhsT=ident_bf16[:], rhs=beta_sb[:, cols], start=False, stop=True)
+                nc.scalar.copy(out=o, in_=total[:])
+            for n in range(0, len(own), 2):
+                for piece in own[n : n + 2]:
+                    subtract_mean_and_scale(*piece)
+                for piece in own[n : n + 2]:
+                    normalise_and_store(*piece)
+                if n == 2:
+                    o, cols = part_of(c, slice(shared[0].start, shared[-1].stop))[1:]
+                    nc.sync.dma_start(out=out_view[:, b, cols], in_=o)

@@ -186,12 +186,13 @@ def tile_multiheadattn_pb_t_kernel(tc, h_attn, Wo, bo, x, gamma, beta, out):
                     )
                 acc_of[(c, j)] = acc
 
-        def add_bias_and_residual(c):
+        def add_bias_and_residual(c, tiles=ALL_TILES):
             if c < OTHERS_ADD_FROM:
+                cols = slice(tiles.start * D_OUT, tiles.stop * D_OUT)
                 nc.vector.tensor_tensor(
-                    out=o_tiles[c // CHUNKS_PER_BATCH][:, chunk_cols(c, CHUNK_D)],
-                    in0=bo_in[c][:],
-                    in1=x_in[c][:],
+                    out=o_tiles[c // CHUNKS_PER_BATCH][:, chunk_cols(c, CHUNK_D)][:, cols],
+                    in0=bo_in[c][:, cols],
+                    in1=x_in[c][:, cols],
                     op=ADD,
                 )
                 return
@@ -332,15 +333,16 @@ def tile_multiheadattn_pb_t_kernel(tc, h_attn, Wo, bo, x, gamma, beta, out):
                 load(i + INPUT_BUFS)
             if is_chunk(i + 2):
                 transpose(i + 2, ALL_TILES)
-            if is_chunk(i + 1):
-                for half in (FIRST_HALF, SECOND_HALF) if done == 0 else (ALL_TILES,):
-                    quantise(i + 1, half)
+            if done > 0 and is_chunk(i + 1):
+                quantise(i + 1, ALL_TILES)
             new_statistics = done % CHUNKS_PER_BATCH == 0
             if not new_statistics:
                 subtract_mean_and_scale(done, whole)
             if is_chunk(i + 1):
                 add_bias_and_residual(i + 1)
             add_projection(i)
+            if done == 0:
+                quantise(i + 1, ALL_TILES)
             if new_statistics:
                 for half in halves:
                     subtract_mean_and_scale(done, half)
@@ -365,10 +367,9 @@ def tile_multiheadattn_pb_t_kernel(tc, h_attn, Wo, bo, x, gamma, beta, out):
             load_bias_and_residual(0)
             load(1)
             load(2)
-            load_h(3, ALL_TILES)
+            load(3)
             nc.sync.dma_start(out=gamma_sb[:], in_=gamma_view)
             nc.sync.dma_start(out=beta_sb[:], in_=beta_view)
-            load_bias_and_residual(3)
             load(4)
             transpose(0, FIRST_HALF)
             regroup_wo(0)
@@ -391,13 +392,15 @@ def tile_multiheadattn_pb_t_kernel(tc, h_attn, Wo, bo, x, gamma, beta, out):
                 project(1, slice(j, j + 1))
                 square_tile(0, j)
             load(5)
-            add_bias_and_residual(2)
+            add_bias_and_residual(2, FIRST_HALF)
             add_projection(1)
             for half in (FIRST_HALF, SECOND_HALF):
                 quantise(2, half)
-            transpose(3, ALL_TILES)
+            add_bias_and_residual(2, SECOND_HALF)
+            transpose(3, FIRST_HALF)
             project(2, ALL_TILES)
             squares(1)
+            transpose(3, SECOND_HALF)
             moments(0)
             tensor_add_bias_and_residual(3)
             load(6)

@@ -36,6 +36,8 @@ STAGE_BUFS = 3
 
 OTHERS_ADD_FROM = 3
 GPSIMD_ADD_TILES = 2
+GPSIMD_COLS = slice(0, 832)
+VECTOR_COLS = slice(828, GPSIMD_ADD_TILES * D_OUT)
 TENSOR_NORM_TILES = 2
 ALL_TILES = slice(0, CHUNK_TILES)
 FIRST_HALF = slice(0, HALF_TILES)
@@ -85,6 +87,8 @@ def tile_multiheadattn_pb_t_kernel(tc, h_attn, Wo, bo, x, gamma, beta, out):
         gap_square = const.tile([P, BATCH], F32)
         std = const.tile([P, BATCH], F32)
         rstd = const.tile([P, BATCH], F32)
+
+        nc.scalar.activation(out=std[:, :1], in_=eps_part[:], func=FUNC.Sqrt)
 
         o_tiles = [const.tile([P, BATCH_D], F32, name="o%d" % b) for b in range(BATCH)]
         gamma_sb = const.tile([P, BATCH_D], BF16)
@@ -197,10 +201,8 @@ def tile_multiheadattn_pb_t_kernel(tc, h_attn, Wo, bo, x, gamma, beta, out):
                 )
                 return
             bx = gpsimd_pool.tile([P, GPSIMD_ADD_TILES * D_OUT], F32)
-            rest = slice(896, GPSIMD_ADD_TILES * D_OUT)
-            nc.vector.tensor_tensor(out=bx[:, rest], in0=bo_in[c][:, rest], in1=x_in[c][:, rest], op=ADD)
-            nc.vector.memset(bx[:, :1], 0.0)
-            nc.gpsimd.tensor_tensor(out=bx[:, :896], in0=bo_in[c][:, :896], in1=x_in[c][:, :896], op=ADD)
+            for engine, cols in ((nc.vector, VECTOR_COLS), (nc.gpsimd, GPSIMD_COLS)):
+                engine.tensor_tensor(out=bx[:, cols], in0=bo_in[c][:, cols], in1=x_in[c][:, cols], op=ADD)
             gpsimd_sum_of[c] = bx
 
         def tensor_add_bias_and_residual(c):

@@ -36,6 +36,7 @@ STAGE_BUFS = 3
 
 OTHERS_ADD_FROM = 3
 GPSIMD_ADD_TILES = 2
+LAST_SUM_TILES = 1
 GPSIMD_COLS = slice(0, 832)
 VECTOR_COLS = slice(828, GPSIMD_ADD_TILES * D_OUT)
 TENSOR_NORM_TILES = 2
@@ -64,10 +65,11 @@ def tile_multiheadattn_pb_t_kernel(tc, h_attn, Wo, bo, x, gamma, beta, out):
         grouped_pool = ctx.enter_context(tc.tile_pool(name="grouped_pool", bufs=STAGE_BUFS))
         mx_pool = ctx.enter_context(tc.tile_pool(name="mx_pool", bufs=STAGE_BUFS))
         scratch_pool = ctx.enter_context(tc.tile_pool(name="scratch_pool", bufs=4))
+        sum_pool = ctx.enter_context(tc.tile_pool(name="sum_pool", bufs=1))
         gpsimd_pool = ctx.enter_context(tc.tile_pool(name="gpsimd_pool", bufs=2))
-        psum_xt = ctx.enter_context(tc.psum_pool(name="psum_xt", bufs=2))
-        psum_acc = ctx.enter_context(tc.psum_pool(name="psum_acc", bufs=CHUNK_TILES))
-        psum_plain = ctx.enter_context(tc.psum_pool(name="psum_plain", bufs=2))
+        psum_xt = ctx.enter_context(tc.psum_pool(name="psum_xt", bufs=3))
+        psum_acc = ctx.enter_context(tc.psum_pool(name="psum_acc", bufs=4))
+        psum_plain = ctx.enter_context(tc.psum_pool(name="psum_plain", bufs=1))
 
         ident = const.tile([P, P], F32)
         make_identity(nc, ident[:])
@@ -131,13 +133,14 @@ def tile_multiheadattn_pb_t_kernel(tc, h_attn, Wo, bo, x, gamma, beta, out):
             chunk = h_view[:, c // CHUNKS_PER_BATCH, chunk_cols(c, CHUNK_K)]
             nc.sync.dma_start(out=h_in[c][:, cols], in_=chunk[:, cols])
 
-        def load_bias_and_residual(c):
-            b = c // CHUNKS_PER_BATCH
-            bo_sb = add_pool.tile([P, CHUNK_D], BF16)
-            nc.sync.dma_start(out=bo_sb[:], in_=bo_view[:, b, chunk_cols(c, CHUNK_D)])
-            x_sb = add_pool.tile([P, CHUNK_D], BF16)
-            nc.sync.dma_start(out=x_sb[:], in_=x_view[:, b, chunk_cols(c, CHUNK_D)])
-            bo_in[c], x_in[c] = bo_sb, x_sb
+        def load_bias_and_residual(c, tiles=ALL_TILES):
+            if tiles.start == 0:
+                bo_in[c] = add_pool.tile([P, CHUNK_D], BF16, name="bo_sb")
+                x_in[c] = add_pool.tile([P, CHUNK_D], BF16, name="x_sb")
+            cols = slice(tiles.start * D_OUT, tiles.stop * D_OUT)
+            for view, tile in ((bo_view, bo_in[c]), (x_view, x_in[c])):
+                chunk = view[:, c // CHUNKS_PER_BATCH, chunk_cols(c, CHUNK_D)]
+                nc.sync.dma_start(out=tile[:, cols], in_=chunk[:, cols])
 
         def load(c):
             load_h(c, ALL_TILES)
@@ -209,19 +212,44 @@ def tile_multiheadattn_pb_t_kernel(tc, h_attn, Wo, bo, x, gamma, beta, out):
             if c < OTHERS_ADD_FROM:
                 return
             o_chunk = o_tiles[c // CHUNKS_PER_BATCH][:, chunk_cols(c, CHUNK_D)]
-            for j in range(GPSIMD_ADD_TILES, CHUNK_TILES):
+            for j in range(GPSIMD_ADD_TILES, vector_tiles(c)):
                 cols = slice(j * D_OUT, (j + 1) * D_OUT)
                 bx = psum_plain.tile([P, D_OUT], F32, tag="plain")
                 nc.tensor.matmul(bx[:], lhsT=ident_bf16[:], rhs=bo_in[c][:, cols], start=True, stop=False)
                 nc.tensor.matmul(bx[:], lhsT=ident_bf16[:], rhs=x_in[c][:, cols], start=False, stop=True)
                 nc.scalar.copy(out=o_chunk[:, cols], in_=bx[:])
 
+        def vector_tiles(c):
+            return CHUNK_TILES - LAST_SUM_TILES if c == CHUNKS - 1 else CHUNK_TILES
+
+        def copy_projection(c):
+            for j in range(vector_tiles(c), CHUNK_TILES):
+                acc_sb = sum_pool.tile([P, D_OUT], F32)
+                nc.scalar.copy(out=acc_sb[:], in_=acc_of[(c, j)][:])
+                acc_of[(c, j)] = acc_sb
+
+        def tensor_sum(c):
+            o_chunk = o_tiles[c // CHUNKS_PER_BATCH][:, chunk_cols(c, CHUNK_D)]
+            for j in range(vector_tiles(c), CHUNK_TILES):
+                cols = slice(j * D_OUT, (j + 1) * D_OUT)
+                column = stats_column(c, j)
+                total = psum_plain.tile([P, D_OUT], F32, tag="plain")
+                nc.tensor.matmul(total[:], lhsT=ident_bf16[:], rhs=bo_in[c][:, cols], start=True, stop=False)
+                nc.tensor.matmul(total[:], lhsT=ident_bf16[:], rhs=x_in[c][:, cols], start=False, stop=False)
+                nc.tensor.matmul(total[:], lhsT=ident[:], rhs=acc_of[(c, j)][:], start=False, stop=True)
+                nc.scalar.activation(
+                    out=o_chunk[:, cols],
+                    in_=total[:],
+                    func=FUNC.Copy,
+                    accum_out=stats[:, column : column + 1],
+                )
+
         def stats_column(c, j):
             return (c // CHUNKS_PER_BATCH) * STATS + (c % CHUNKS_PER_BATCH) * CHUNK_TILES + j
 
         def add_projection(c):
             o_chunk = o_tiles[c // CHUNKS_PER_BATCH][:, chunk_cols(c, CHUNK_D)]
-            for j in range(CHUNK_TILES):
+            for j in range(vector_tiles(c)):
                 cols = slice(j * D_OUT, (j + 1) * D_OUT)
                 o_tile = o_chunk[:, cols]
                 in_gpsimd_sum = c in gpsimd_sum_of and j < GPSIMD_ADD_TILES
@@ -237,7 +265,7 @@ def tile_multiheadattn_pb_t_kernel(tc, h_attn, Wo, bo, x, gamma, beta, out):
                 )
 
         def totals_of(first, width):
-            totals = psum_plain.tile([P, STATS], F32, tag="plain")
+            totals = psum_xt.tile([P, STATS], F32, tag="xt")
             nc.tensor.matmul(
                 totals[:, :width], lhsT=ones[:], rhs=stats[:, first : first + width], start=True, stop=True
             )
@@ -338,23 +366,27 @@ def tile_multiheadattn_pb_t_kernel(tc, h_attn, Wo, bo, x, gamma, beta, out):
             if done > 0 and is_chunk(i + 1):
                 quantise(i + 1, ALL_TILES)
             new_statistics = done % CHUNKS_PER_BATCH == 0
-            if not new_statistics:
+            additions_first = new_statistics or i == CHUNKS - 1
+            if not additions_first:
                 subtract_mean_and_scale(done, whole)
             if is_chunk(i + 1):
                 add_bias_and_residual(i + 1)
             add_projection(i)
             if done == 0:
                 quantise(i + 1, ALL_TILES)
-            if new_statistics:
+            if additions_first:
                 for half in halves:
                     subtract_mean_and_scale(done, half)
+            if new_statistics:
                 reciprocal(done // CHUNKS_PER_BATCH)
-            for part in halves if new_statistics else [whole]:
+            for part in halves if additions_first else [whole]:
                 normalise_and_store(done, part)
+            tensor_sum(i)
             if i % CHUNKS_PER_BATCH == 0:
                 shift(i // CHUNKS_PER_BATCH)
             if is_chunk(i + 1):
                 project(i + 1, ALL_TILES)
+                copy_projection(i + 1)
             squares(i)
             if i % CHUNKS_PER_BATCH == CHUNKS_PER_BATCH - 1:
                 moments(i // CHUNKS_PER_BATCH)
@@ -363,12 +395,15 @@ def tile_multiheadattn_pb_t_kernel(tc, h_attn, Wo, bo, x, gamma, beta, out):
 
         with tc.manual_schedule():
             load_h(0, FIRST_HALF)
-            for g in range(PASSES):
-                load_wo(g)
+            load_wo(0)
+            load_wo(1)
+            load_bias_and_residual(0, FIRST_HALF)
             load_h(0, SECOND_HALF)
-            load_bias_and_residual(0)
-            load(1)
-            load(2)
+            load_bias_and_residual(0, SECOND_HALF)
+            load_h(1, ALL_TILES)
+            load_bias_and_residual(1)
+            load_h(2, ALL_TILES)
+            load_bias_and_residual(2)
             load(3)
             nc.sync.dma_start(out=gamma_sb[:], in_=gamma_view)
             nc.sync.dma_start(out=beta_sb[:], in_=beta_view)
@@ -376,23 +411,32 @@ def tile_multiheadattn_pb_t_kernel(tc, h_attn, Wo, bo, x, gamma, beta, out):
             transpose(0, FIRST_HALF)
             regroup_wo(0)
             quantise(0, FIRST_HALF)
-            regroup_wo(1)
-            for g in range(PASSES):
-                quantise_wo(g)
+            nc.scalar.copy(out=wo_grouped_cti[:, 1], in_=wo_raw_cti[:, 1])
+            quantise_wo(0)
+            add_bias_and_residual(0, FIRST_HALF)
+            quantise_wo(1)
             transpose(0, SECOND_HALF)
+            add_bias_and_residual(0, SECOND_HALF)
             quantise(0, SECOND_HALF)
-            add_bias_and_residual(0)
             project(0, ALL_TILES)
             transpose(1, ALL_TILES)
             add_projection(0)
             shift(0)
             for half in (FIRST_HALF, SECOND_HALF):
                 quantise(1, half)
-            add_bias_and_residual(1)
-            for j in range(CHUNK_TILES):
-                transpose(2, slice(j, j + 1))
-                project(1, slice(j, j + 1))
-                square_tile(0, j)
+                add_bias_and_residual(1, half)
+            project(1, slice(0, 1))
+            transpose(2, slice(0, 1))
+            square_tile(0, 0)
+            project(1, slice(1, 2))
+            transpose(2, slice(1, 2))
+            square_tile(0, 1)
+            project(1, slice(2, 3))
+            transpose(2, slice(2, 3))
+            square_tile(0, 2)
+            project(1, slice(3, 4))
+            transpose(2, slice(3, 4))
+            square_tile(0, 3)
             load(5)
             add_bias_and_residual(2, FIRST_HALF)
             add_projection(1)
@@ -418,7 +462,7 @@ def tile_multiheadattn_pb_t_kernel(tc, h_attn, Wo, bo, x, gamma, beta, out):
                 subtract_mean_and_scale(c, tile)
             for tile in shared:
                 o, cols = part_of(c, tile)[1:]
-                total = psum_plain.tile([P, D_OUT], F32, tag="plain")
+                total = psum_acc.tile([P, D_OUT], F32, tag="acc")
                 nc.tensor.matmul(total[:], lhsT=diagonal[:], rhs=o, start=True, stop=False)
                 nc.tensor.matmul(total[:], lhsT=ident_bf16[:], rhs=beta_sb[:, cols], start=False, stop=True)
                 nc.scalar.copy(out=o, in_=total[:])

@@ -29,6 +29,7 @@ WORDS = K_DIM // 2
 PLANES = WORDS // P
 TILE_CODES = K_DIM // PACK
 HALF_TILES = CHUNK_TILES // 2
+FEATURE_BLOCKS = D_OUT // P
 COUNT = SEQ * D_OUT
 
 INPUT_BUFS = 5
@@ -36,9 +37,9 @@ STAGE_BUFS = 3
 
 OTHERS_ADD_FROM = 3
 GPSIMD_ADD_TILES = 2
-LAST_SUM_TILES = 1
-GPSIMD_COLS = slice(0, 832)
-VECTOR_COLS = slice(828, GPSIMD_ADD_TILES * D_OUT)
+TENSOR_SUM_TILES = 2
+GPSIMD_COLS = slice(0, 416)
+VECTOR_COLS = slice(412, GPSIMD_ADD_TILES * D_OUT)
 TENSOR_NORM_TILES = 2
 ALL_TILES = slice(0, CHUNK_TILES)
 FIRST_HALF = slice(0, HALF_TILES)
@@ -65,11 +66,11 @@ def tile_multiheadattn_pb_t_kernel(tc, h_attn, Wo, bo, x, gamma, beta, out):
         grouped_pool = ctx.enter_context(tc.tile_pool(name="grouped_pool", bufs=STAGE_BUFS))
         mx_pool = ctx.enter_context(tc.tile_pool(name="mx_pool", bufs=STAGE_BUFS))
         scratch_pool = ctx.enter_context(tc.tile_pool(name="scratch_pool", bufs=4))
-        sum_pool = ctx.enter_context(tc.tile_pool(name="sum_pool", bufs=1))
+        sum_pool = ctx.enter_context(tc.tile_pool(name="sum_pool", bufs=2))
         gpsimd_pool = ctx.enter_context(tc.tile_pool(name="gpsimd_pool", bufs=2))
-        psum_xt = ctx.enter_context(tc.psum_pool(name="psum_xt", bufs=3))
+        psum_xt = ctx.enter_context(tc.psum_pool(name="psum_xt", bufs=2))
         psum_acc = ctx.enter_context(tc.psum_pool(name="psum_acc", bufs=4))
-        psum_plain = ctx.enter_context(tc.psum_pool(name="psum_plain", bufs=1))
+        psum_plain = ctx.enter_context(tc.psum_pool(name="psum_plain", bufs=2))
 
         ident = const.tile([P, P], F32)
         make_identity(nc, ident[:])
@@ -179,6 +180,23 @@ def tile_multiheadattn_pb_t_kernel(tc, h_attn, Wo, bo, x, gamma, beta, out):
         def project(c, tiles):
             for j in range(tiles.start, tiles.stop):
                 acc = psum_acc.tile([P, D_OUT], F32)
+                acc_of[(c, j)] = acc
+                if j >= vector_tiles(c):
+                    for f in range(FEATURE_BLOCKS):
+                        block = slice(f * P, (f + 1) * P)
+                        for g in range(PASSES):
+                            tokens = slice((j * PASSES + g) * P, (j * PASSES + g + 1) * P)
+                            features = slice(g * D_OUT + f * P, g * D_OUT + (f + 1) * P)
+                            nc.tensor.matmul_mx(
+                                out=acc[:, block],
+                                lhsT=wo_codes[:, features].bitcast(FP8X4),
+                                lhsT_scale=wo_scales[:, features],
+                                rhs=h_codes[c][:, tokens].bitcast(FP8X4),
+                                rhs_scale=h_scales[c][:, tokens],
+                                start=(g == 0),
+                                stop=(g == PASSES - 1),
+                            )
+                    continue
                 for g in range(PASSES):
                     tokens = slice((j * PASSES + g) * P, (j * PASSES + g + 1) * P)
                     features = slice(g * D_OUT, (g + 1) * D_OUT)
@@ -191,7 +209,6 @@ def tile_multiheadattn_pb_t_kernel(tc, h_attn, Wo, bo, x, gamma, beta, out):
                         start=(g == 0),
                         stop=(g == PASSES - 1),
                     )
-                acc_of[(c, j)] = acc
 
         def add_bias_and_residual(c, tiles=ALL_TILES):
             if c < OTHERS_ADD_FROM:
@@ -208,19 +225,8 @@ def tile_multiheadattn_pb_t_kernel(tc, h_attn, Wo, bo, x, gamma, beta, out):
                 engine.tensor_tensor(out=bx[:, cols], in0=bo_in[c][:, cols], in1=x_in[c][:, cols], op=ADD)
             gpsimd_sum_of[c] = bx
 
-        def tensor_add_bias_and_residual(c):
-            if c < OTHERS_ADD_FROM:
-                return
-            o_chunk = o_tiles[c // CHUNKS_PER_BATCH][:, chunk_cols(c, CHUNK_D)]
-            for j in range(GPSIMD_ADD_TILES, vector_tiles(c)):
-                cols = slice(j * D_OUT, (j + 1) * D_OUT)
-                bx = psum_plain.tile([P, D_OUT], F32, tag="plain")
-                nc.tensor.matmul(bx[:], lhsT=ident_bf16[:], rhs=bo_in[c][:, cols], start=True, stop=False)
-                nc.tensor.matmul(bx[:], lhsT=ident_bf16[:], rhs=x_in[c][:, cols], start=False, stop=True)
-                nc.scalar.copy(out=o_chunk[:, cols], in_=bx[:])
-
         def vector_tiles(c):
-            return CHUNK_TILES - LAST_SUM_TILES if c == CHUNKS - 1 else CHUNK_TILES
+            return CHUNK_TILES - TENSOR_SUM_TILES if c >= OTHERS_ADD_FROM else CHUNK_TILES
 
         def copy_projection(c):
             for j in range(vector_tiles(c), CHUNK_TILES):
@@ -236,7 +242,16 @@ def tile_multiheadattn_pb_t_kernel(tc, h_attn, Wo, bo, x, gamma, beta, out):
                 total = psum_plain.tile([P, D_OUT], F32, tag="plain")
                 nc.tensor.matmul(total[:], lhsT=ident_bf16[:], rhs=bo_in[c][:, cols], start=True, stop=False)
                 nc.tensor.matmul(total[:], lhsT=ident_bf16[:], rhs=x_in[c][:, cols], start=False, stop=False)
-                nc.tensor.matmul(total[:], lhsT=ident[:], rhs=acc_of[(c, j)][:], start=False, stop=True)
+                for f in range(FEATURE_BLOCKS):
+                    block = slice(f * P, (f + 1) * P)
+                    nc.tensor.matmul(
+                        total[:, block],
+                        lhsT=acc_of[(c, j)][:, block],
+                        rhs=ident[:],
+                        start=False,
+                        stop=(f == FEATURE_BLOCKS - 1),
+                        is_transpose=True,
+                    )
                 nc.scalar.activation(
                     out=o_chunk[:, cols],
                     in_=total[:],
@@ -390,8 +405,6 @@ def tile_multiheadattn_pb_t_kernel(tc, h_attn, Wo, bo, x, gamma, beta, out):
             squares(i)
             if i % CHUNKS_PER_BATCH == CHUNKS_PER_BATCH - 1:
                 moments(i // CHUNKS_PER_BATCH)
-            if is_chunk(i + 2):
-                tensor_add_bias_and_residual(i + 2)
 
         with tc.manual_schedule():
             load_h(0, FIRST_HALF)
@@ -448,7 +461,6 @@ def tile_multiheadattn_pb_t_kernel(tc, h_attn, Wo, bo, x, gamma, beta, out):
             squares(1)
             transpose(3, SECOND_HALF)
             moments(0)
-            tensor_add_bias_and_residual(3)
             load(6)
             for i in range(CHUNKS_PER_BATCH, CHUNKS):
                 step(i)

@@ -35,11 +35,12 @@ COUNT = SEQ * D_OUT
 INPUT_BUFS = 5
 STAGE_BUFS = 3
 
-OTHERS_ADD_FROM = 3
+OTHERS_ADD_FROM = 4
+TENSOR_SUM_FROM = 3
 GPSIMD_ADD_TILES = 2
+NORM_LAG = 2
 TENSOR_SUM_TILES = 2
-GPSIMD_COLS = slice(0, 416)
-VECTOR_COLS = slice(412, GPSIMD_ADD_TILES * D_OUT)
+G_COLS = 416
 TENSOR_NORM_TILES = 2
 ALL_TILES = slice(0, CHUNK_TILES)
 FIRST_HALF = slice(0, HALF_TILES)
@@ -67,9 +68,8 @@ def tile_multiheadattn_pb_t_kernel(tc, h_attn, Wo, bo, x, gamma, beta, out):
         mx_pool = ctx.enter_context(tc.tile_pool(name="mx_pool", bufs=STAGE_BUFS))
         scratch_pool = ctx.enter_context(tc.tile_pool(name="scratch_pool", bufs=4))
         sum_pool = ctx.enter_context(tc.tile_pool(name="sum_pool", bufs=2))
-        gpsimd_pool = ctx.enter_context(tc.tile_pool(name="gpsimd_pool", bufs=2))
         psum_xt = ctx.enter_context(tc.psum_pool(name="psum_xt", bufs=2))
-        psum_acc = ctx.enter_context(tc.psum_pool(name="psum_acc", bufs=4))
+        psum_acc = ctx.enter_context(tc.psum_pool(name="psum_acc", bufs=1))
         psum_plain = ctx.enter_context(tc.psum_pool(name="psum_plain", bufs=2))
 
         ident = const.tile([P, P], F32)
@@ -121,7 +121,7 @@ def tile_multiheadattn_pb_t_kernel(tc, h_attn, Wo, bo, x, gamma, beta, out):
 
         h_in, bo_in, x_in = {}, {}, {}
         h_grouped, h_codes, h_scales = {}, {}, {}
-        acc_of, gpsimd_sum_of = {}, {}
+        acc_of = {}
 
         def chunk_cols(c, width):
             half = c % CHUNKS_PER_BATCH
@@ -179,7 +179,7 @@ def tile_multiheadattn_pb_t_kernel(tc, h_attn, Wo, bo, x, gamma, beta, out):
 
         def project(c, tiles):
             for j in range(tiles.start, tiles.stop):
-                acc = psum_acc.tile([P, D_OUT], F32)
+                acc = psum_acc.tile([P, D_OUT], F32, tag="acc%d" % ((j + 2 * c) % CHUNK_TILES))
                 acc_of[(c, j)] = acc
                 if j >= vector_tiles(c):
                     for f in range(FEATURE_BLOCKS):
@@ -210,33 +210,32 @@ def tile_multiheadattn_pb_t_kernel(tc, h_attn, Wo, bo, x, gamma, beta, out):
                         stop=(g == PASSES - 1),
                     )
 
-        def add_bias_and_residual(c, tiles=ALL_TILES):
-            if c < OTHERS_ADD_FROM:
-                cols = slice(tiles.start * D_OUT, tiles.stop * D_OUT)
-                nc.vector.tensor_tensor(
-                    out=o_tiles[c // CHUNKS_PER_BATCH][:, chunk_cols(c, CHUNK_D)][:, cols],
-                    in0=bo_in[c][:, cols],
-                    in1=x_in[c][:, cols],
-                    op=ADD,
+        def add_bias_and_residual(c, cols):
+            engine_of = nc.vector
+            o_chunk = o_tiles[c // CHUNKS_PER_BATCH][:, chunk_cols(c, CHUNK_D)]
+            engine_of.tensor_tensor(
+                out=o_chunk[:, cols], in0=bo_in[c][:, cols], in1=x_in[c][:, cols], op=ADD
+            )
+
+        def share_bias_and_residual(c, gpsimd_cols, vector_cols):
+            o_chunk = o_tiles[c // CHUNKS_PER_BATCH][:, chunk_cols(c, CHUNK_D)]
+            for engine, cols in ((nc.vector, vector_cols), (nc.gpsimd, gpsimd_cols)):
+                engine.tensor_tensor(
+                    out=o_chunk[:, cols], in0=bo_in[c][:, cols], in1=x_in[c][:, cols], op=ADD
                 )
-                return
-            bx = gpsimd_pool.tile([P, GPSIMD_ADD_TILES * D_OUT], F32)
-            for engine, cols in ((nc.vector, VECTOR_COLS), (nc.gpsimd, GPSIMD_COLS)):
-                engine.tensor_tensor(out=bx[:, cols], in0=bo_in[c][:, cols], in1=x_in[c][:, cols], op=ADD)
-            gpsimd_sum_of[c] = bx
 
         def vector_tiles(c):
-            return CHUNK_TILES - TENSOR_SUM_TILES if c >= OTHERS_ADD_FROM else CHUNK_TILES
+            return CHUNK_TILES - TENSOR_SUM_TILES if c >= TENSOR_SUM_FROM else CHUNK_TILES
 
-        def copy_projection(c):
-            for j in range(vector_tiles(c), CHUNK_TILES):
+        def copy_projection(c, tiles=ALL_TILES):
+            for j in range(max(tiles.start, vector_tiles(c)), tiles.stop):
                 acc_sb = sum_pool.tile([P, D_OUT], F32)
                 nc.scalar.copy(out=acc_sb[:], in_=acc_of[(c, j)][:])
                 acc_of[(c, j)] = acc_sb
 
-        def tensor_sum(c):
+        def tensor_sum(c, tiles=ALL_TILES):
             o_chunk = o_tiles[c // CHUNKS_PER_BATCH][:, chunk_cols(c, CHUNK_D)]
-            for j in range(vector_tiles(c), CHUNK_TILES):
+            for j in range(max(tiles.start, vector_tiles(c)), tiles.stop):
                 cols = slice(j * D_OUT, (j + 1) * D_OUT)
                 column = stats_column(c, j)
                 total = psum_plain.tile([P, D_OUT], F32, tag="plain")
@@ -267,13 +266,12 @@ def tile_multiheadattn_pb_t_kernel(tc, h_attn, Wo, bo, x, gamma, beta, out):
             for j in range(vector_tiles(c)):
                 cols = slice(j * D_OUT, (j + 1) * D_OUT)
                 o_tile = o_chunk[:, cols]
-                in_gpsimd_sum = c in gpsimd_sum_of and j < GPSIMD_ADD_TILES
                 column = stats_column(c, j)
                 nc.vector.scalar_tensor_tensor(
                     out=o_tile,
                     in0=acc_of[(c, j)][:],
                     scalar=0.0,
-                    in1=gpsimd_sum_of[c][:, cols] if in_gpsimd_sum else o_tile,
+                    in1=o_tile,
                     op0=ADD,
                     op1=ADD,
                     accum_out=stats[:, column : column + 1],
@@ -287,7 +285,7 @@ def tile_multiheadattn_pb_t_kernel(tc, h_attn, Wo, bo, x, gamma, beta, out):
             return totals
 
         def shift(b):
-            first = b * STATS
+            first = stats_column(b * CHUNKS_PER_BATCH, 0)
             totals = totals_of(first, 1)
             nc.scalar.activation(
                 out=neg_shift[:, b : b + 1], in_=totals[:, :1], func=FUNC.Copy, scale=-1.0 / (P * D_OUT)
@@ -372,39 +370,61 @@ def tile_multiheadattn_pb_t_kernel(tc, h_attn, Wo, bo, x, gamma, beta, out):
         whole = slice(0, CHUNK_D)
         halves = [slice(0, CHUNK_D // 2), slice(CHUNK_D // 2, CHUNK_D)]
 
+        def normalise_1(half):
+            subtract_mean_and_scale(half // 2, halves[half % 2])
+
+        def normalise_2(half):
+            normalise_and_store(half // 2, halves[half % 2])
+
+        def norm_halves(i):
+            return [2 * i - 5, 2 * i - 4] if i > 3 else [2]
+
         def step(i):
-            done = i - CHUNKS_PER_BATCH
-            if is_chunk(i + INPUT_BUFS):
-                load(i + INPUT_BUFS)
-            if is_chunk(i + 2):
-                transpose(i + 2, ALL_TILES)
-            if done > 0 and is_chunk(i + 1):
-                quantise(i + 1, ALL_TILES)
-            new_statistics = done % CHUNKS_PER_BATCH == 0
-            additions_first = new_statistics or i == CHUNKS - 1
-            if not additions_first:
-                subtract_mean_and_scale(done, whole)
+            one = [slice(j, j + 1) for j in range(CHUNK_TILES)]
+
+            def bring(c, j):
+                if is_chunk(c):
+                    transpose(c, one[j])
+
+            early, late = norm_halves(i), []
+            if i % CHUNKS_PER_BATCH == 0:
+                early, late = early[:1], early[1:]
+            for half in early:
+                normalise_1(half)
+            project(i, one[0])
+            if i % CHUNKS_PER_BATCH == 1:
+                bring(i + 1, 2)
+            project(i, one[1])
+            if i % CHUNKS_PER_BATCH == 0:
+                moments(i // CHUNKS_PER_BATCH - 1)
+                bring(i + 1, 2)
+            bring(i + 1, 3)
             if is_chunk(i + 1):
-                add_bias_and_residual(i + 1)
+                share_bias_and_residual(i + 1, slice(0, G_COLS), slice(G_COLS - 4, 1024))
             add_projection(i)
-            if done == 0:
-                quantise(i + 1, ALL_TILES)
-            if additions_first:
-                for half in halves:
-                    subtract_mean_and_scale(done, half)
-            if new_statistics:
-                reciprocal(done // CHUNKS_PER_BATCH)
-            for part in halves if additions_first else [whole]:
-                normalise_and_store(done, part)
-            tensor_sum(i)
+            project(i, one[2])
+            copy_projection(i, one[2])
+            bring(i + 2, 0)
+            project(i, one[3])
+            copy_projection(i, one[3])
             if i % CHUNKS_PER_BATCH == 0:
                 shift(i // CHUNKS_PER_BATCH)
+            square_tile(i, 0)
+            square_tile(i, 1)
+            tensor_sum(i, one[2])
+            bring(i + 2, 1)
+            for half in early:
+                normalise_2(half)
+            for half in late:
+                reciprocal(half // 4)
+                normalise_1(half)
             if is_chunk(i + 1):
-                project(i + 1, ALL_TILES)
-                copy_projection(i + 1)
-            squares(i)
-            if i % CHUNKS_PER_BATCH == CHUNKS_PER_BATCH - 1:
-                moments(i // CHUNKS_PER_BATCH)
+                quantise(i + 1, ALL_TILES)
+            for half in late:
+                normalise_2(half)
+            tensor_sum(i, one[3])
+            for j in (2, 3):
+                square_tile(i, j)
 
         with tc.manual_schedule():
             load_h(0, FIRST_HALF)
@@ -417,19 +437,19 @@ def tile_multiheadattn_pb_t_kernel(tc, h_attn, Wo, bo, x, gamma, beta, out):
             load_bias_and_residual(1)
             load_h(2, ALL_TILES)
             load_bias_and_residual(2)
-            load(3)
             nc.sync.dma_start(out=gamma_sb[:], in_=gamma_view)
             nc.sync.dma_start(out=beta_sb[:], in_=beta_view)
+            load(3)
             load(4)
             transpose(0, FIRST_HALF)
             regroup_wo(0)
             quantise(0, FIRST_HALF)
             nc.scalar.copy(out=wo_grouped_cti[:, 1], in_=wo_raw_cti[:, 1])
             quantise_wo(0)
-            add_bias_and_residual(0, FIRST_HALF)
+            add_bias_and_residual(0, slice(0, 1024))
             quantise_wo(1)
             transpose(0, SECOND_HALF)
-            add_bias_and_residual(0, SECOND_HALF)
+            add_bias_and_residual(0, slice(1024, 2048))
             quantise(0, SECOND_HALF)
             project(0, ALL_TILES)
             transpose(1, ALL_TILES)
@@ -437,7 +457,7 @@ def tile_multiheadattn_pb_t_kernel(tc, h_attn, Wo, bo, x, gamma, beta, out):
             shift(0)
             for half in (FIRST_HALF, SECOND_HALF):
                 quantise(1, half)
-                add_bias_and_residual(1, half)
+                add_bias_and_residual(1, halves[0] if half == FIRST_HALF else halves[1])
             project(1, slice(0, 1))
             transpose(2, slice(0, 1))
             square_tile(0, 0)
@@ -451,19 +471,33 @@ def tile_multiheadattn_pb_t_kernel(tc, h_attn, Wo, bo, x, gamma, beta, out):
             transpose(2, slice(3, 4))
             square_tile(0, 3)
             load(5)
-            add_bias_and_residual(2, FIRST_HALF)
+            share_bias_and_residual(2, slice(0, 832), slice(828, 1024))
             add_projection(1)
             for half in (FIRST_HALF, SECOND_HALF):
                 quantise(2, half)
-            add_bias_and_residual(2, SECOND_HALF)
-            transpose(3, FIRST_HALF)
-            project(2, ALL_TILES)
+            add_bias_and_residual(2, halves[1])
             squares(1)
-            transpose(3, SECOND_HALF)
+            project(2, ALL_TILES)
             moments(0)
+            transpose(3, ALL_TILES)
             load(6)
-            for i in range(CHUNKS_PER_BATCH, CHUNKS):
+            load(7)
+            add_projection(2)
+            shift(1)
+            squares(2)
+            reciprocal(0)
+            for half in halves:
+                subtract_mean_and_scale(0, half)
+            for half in halves:
+                normalise_and_store(0, half)
+            quantise(3, ALL_TILES)
+            add_bias_and_residual(3, halves[0])
+            transpose(4, FIRST_HALF)
+            for i in range(3, CHUNKS):
                 step(i)
+            moments(BATCH - 1)
+            normalise_1(11)
+            normalise_2(11)
             b, c = BATCH - 1, CHUNKS - 1
             tiles = [slice(j * D_OUT, (j + 1) * D_OUT) for j in range(CHUNK_TILES)]
             shared = tiles[CHUNK_TILES - TENSOR_NORM_TILES :]
@@ -474,7 +508,7 @@ def tile_multiheadattn_pb_t_kernel(tc, h_attn, Wo, bo, x, gamma, beta, out):
                 subtract_mean_and_scale(c, tile)
             for tile in shared:
                 o, cols = part_of(c, tile)[1:]
-                total = psum_acc.tile([P, D_OUT], F32, tag="acc")
+                total = psum_acc.tile([P, D_OUT], F32, tag="acc%d" % (cols.start // D_OUT % CHUNK_TILES))
                 nc.tensor.matmul(total[:], lhsT=diagonal[:], rhs=o, start=True, stop=False)
                 nc.tensor.matmul(total[:], lhsT=ident_bf16[:], rhs=beta_sb[:, cols], start=False, stop=True)
                 nc.scalar.copy(out=o, in_=total[:])

@@ -36,7 +36,8 @@ INPUT_BUFS = 5
 STAGE_BUFS = 3
 
 OTHERS_ADD_FROM = 4
-TENSOR_SUM_FROM = 3
+TT = {3: 2, 4: 2, 5: 2, 6: 2, 7: 2}
+GC = {}
 GPSIMD_ADD_TILES = 2
 NORM_LAG = 2
 TENSOR_SUM_TILES = 2
@@ -121,7 +122,7 @@ def tile_multiheadattn_pb_t_kernel(tc, h_attn, Wo, bo, x, gamma, beta, out):
 
         h_in, bo_in, x_in = {}, {}, {}
         h_grouped, h_codes, h_scales = {}, {}, {}
-        acc_of = {}
+        acc_of, total_of = {}, {}
 
         def chunk_cols(c, width):
             half = c % CHUNKS_PER_BATCH
@@ -225,7 +226,7 @@ def tile_multiheadattn_pb_t_kernel(tc, h_attn, Wo, bo, x, gamma, beta, out):
                 )
 
         def vector_tiles(c):
-            return CHUNK_TILES - TENSOR_SUM_TILES if c >= TENSOR_SUM_FROM else CHUNK_TILES
+            return CHUNK_TILES - TT.get(c, 0)
 
         def copy_projection(c, tiles=ALL_TILES):
             for j in range(max(tiles.start, vector_tiles(c)), tiles.stop):
@@ -233,14 +234,20 @@ def tile_multiheadattn_pb_t_kernel(tc, h_attn, Wo, bo, x, gamma, beta, out):
                 nc.scalar.copy(out=acc_sb[:], in_=acc_of[(c, j)][:])
                 acc_of[(c, j)] = acc_sb
 
-        def tensor_sum(c, tiles=ALL_TILES):
-            o_chunk = o_tiles[c // CHUNKS_PER_BATCH][:, chunk_cols(c, CHUNK_D)]
-            for j in range(max(tiles.start, vector_tiles(c)), tiles.stop):
+        def sum_inputs(c):
+            for j in range(vector_tiles(c), CHUNK_TILES):
                 cols = slice(j * D_OUT, (j + 1) * D_OUT)
-                column = stats_column(c, j)
                 total = psum_plain.tile([P, D_OUT], F32, tag="plain")
                 nc.tensor.matmul(total[:], lhsT=ident_bf16[:], rhs=bo_in[c][:, cols], start=True, stop=False)
                 nc.tensor.matmul(total[:], lhsT=ident_bf16[:], rhs=x_in[c][:, cols], start=False, stop=False)
+                total_of[(c, j)] = total
+
+        def sum_projection(c):
+            o_chunk = o_tiles[c // CHUNKS_PER_BATCH][:, chunk_cols(c, CHUNK_D)]
+            for j in range(vector_tiles(c), CHUNK_TILES):
+                cols = slice(j * D_OUT, (j + 1) * D_OUT)
+                column = stats_column(c, j)
+                total = total_of[(c, j)]
                 for f in range(FEATURE_BLOCKS):
                     block = slice(f * P, (f + 1) * P)
                     nc.tensor.matmul(
@@ -377,7 +384,7 @@ def tile_multiheadattn_pb_t_kernel(tc, h_attn, Wo, bo, x, gamma, beta, out):
             normalise_and_store(half // 2, halves[half % 2])
 
         def norm_halves(i):
-            return [2 * i - 5, 2 * i - 4] if i > 3 else [2]
+            return [i - 1] if i < 5 else [2 * i - 6, 2 * i - 5]
 
         def step(i):
             one = [slice(j, j + 1) for j in range(CHUNK_TILES)]
@@ -386,45 +393,33 @@ def tile_multiheadattn_pb_t_kernel(tc, h_attn, Wo, bo, x, gamma, beta, out):
                 if is_chunk(c):
                     transpose(c, one[j])
 
-            early, late = norm_halves(i), []
-            if i % CHUNKS_PER_BATCH == 0:
-                early, late = early[:1], early[1:]
-            for half in early:
+            for half in norm_halves(i):
+                if half % 4 == 0:
+                    reciprocal(half // 4)
                 normalise_1(half)
-            project(i, one[0])
-            if i % CHUNKS_PER_BATCH == 1:
-                bring(i + 1, 2)
-            project(i, one[1])
-            if i % CHUNKS_PER_BATCH == 0:
-                moments(i // CHUNKS_PER_BATCH - 1)
-                bring(i + 1, 2)
+            for j in range(CHUNK_TILES):
+                project(i, one[j])
+                copy_projection(i, one[j])
+            sum_inputs(i)
+            bring(i + 1, 2)
             bring(i + 1, 3)
             if is_chunk(i + 1):
-                share_bias_and_residual(i + 1, slice(0, G_COLS), slice(G_COLS - 4, 1024))
+                g = GC.get(i + 1, 416)
+                share_bias_and_residual(i + 1, slice(0, g), slice(g - 4, vector_tiles(i + 1) * D_OUT))
             add_projection(i)
-            project(i, one[2])
-            copy_projection(i, one[2])
+            sum_projection(i)
+            if i % CHUNKS_PER_BATCH == 0:
+                moments(i // CHUNKS_PER_BATCH - 1)
             bring(i + 2, 0)
-            project(i, one[3])
-            copy_projection(i, one[3])
+            bring(i + 2, 1)
             if i % CHUNKS_PER_BATCH == 0:
                 shift(i // CHUNKS_PER_BATCH)
-            square_tile(i, 0)
-            square_tile(i, 1)
-            tensor_sum(i, one[2])
-            bring(i + 2, 1)
-            for half in early:
+            for j in range(CHUNK_TILES):
+                square_tile(i, j)
+            for half in norm_halves(i):
                 normalise_2(half)
-            for half in late:
-                reciprocal(half // 4)
-                normalise_1(half)
             if is_chunk(i + 1):
                 quantise(i + 1, ALL_TILES)
-            for half in late:
-                normalise_2(half)
-            tensor_sum(i, one[3])
-            for j in (2, 3):
-                square_tile(i, j)
 
         with tc.manual_schedule():
             load_h(0, FIRST_HALF)
@@ -491,13 +486,15 @@ def tile_multiheadattn_pb_t_kernel(tc, h_attn, Wo, bo, x, gamma, beta, out):
             for half in halves:
                 normalise_and_store(0, half)
             quantise(3, ALL_TILES)
-            add_bias_and_residual(3, halves[0])
+            add_bias_and_residual(3, slice(0, vector_tiles(3) * D_OUT))
             transpose(4, FIRST_HALF)
             for i in range(3, CHUNKS):
                 step(i)
             moments(BATCH - 1)
-            normalise_1(11)
-            normalise_2(11)
+            for half in (10, 11):
+                normalise_1(half)
+            for half in (10, 11):
+                normalise_2(half)
             b, c = BATCH - 1, CHUNKS - 1
             tiles = [slice(j * D_OUT, (j + 1) * D_OUT) for j in range(CHUNK_TILES)]
             shared = tiles[CHUNK_TILES - TENSOR_NORM_TILES :]

@@ -36,8 +36,8 @@ INPUT_BUFS = 5
 STAGE_BUFS = 3
 
 OTHERS_ADD_FROM = 4
-TT = {3: 2, 4: 2, 5: 2, 6: 2, 7: 2}
-GC = {}
+TT = {3: 1, 4: 1, 5: 2, 6: 2, 7: 2}
+GC = {4: 700, 5: 700, 6: 416, 7: 416}
 GPSIMD_ADD_TILES = 2
 NORM_LAG = 2
 TENSOR_SUM_TILES = 2
@@ -67,7 +67,7 @@ def tile_multiheadattn_pb_t_kernel(tc, h_attn, Wo, bo, x, gamma, beta, out):
         add_pool = ctx.enter_context(tc.tile_pool(name="add_pool", bufs=INPUT_BUFS))
         grouped_pool = ctx.enter_context(tc.tile_pool(name="grouped_pool", bufs=STAGE_BUFS))
         mx_pool = ctx.enter_context(tc.tile_pool(name="mx_pool", bufs=STAGE_BUFS))
-        scratch_pool = ctx.enter_context(tc.tile_pool(name="scratch_pool", bufs=4))
+        scratch_pool = ctx.enter_context(tc.tile_pool(name="scratch_pool", bufs=1))
         sum_pool = ctx.enter_context(tc.tile_pool(name="sum_pool", bufs=2))
         psum_xt = ctx.enter_context(tc.psum_pool(name="psum_xt", bufs=2))
         psum_acc = ctx.enter_context(tc.psum_pool(name="psum_acc", bufs=1))
@@ -84,6 +84,7 @@ def tile_multiheadattn_pb_t_kernel(tc, h_attn, Wo, bo, x, gamma, beta, out):
 
         STATS = 2 * TILES_PER_BATCH
         stats = const.tile([P, BATCH * STATS], F32)
+        nc.vector.memset(stats[:], 0.0)
         scratch = const.tile([P, BATCH * STATS], F32)
         neg_shift = const.tile([P, BATCH], F32)
         neg_mean = const.tile([P, BATCH], F32)
@@ -225,6 +226,14 @@ def tile_multiheadattn_pb_t_kernel(tc, h_attn, Wo, bo, x, gamma, beta, out):
                     out=o_chunk[:, cols], in0=bo_in[c][:, cols], in1=x_in[c][:, cols], op=ADD
                 )
 
+        def bias_and_residual_on_tensor(c):
+            for j in range(GPSIMD_ADD_TILES, vector_tiles(c)):
+                cols = slice(j * D_OUT, (j + 1) * D_OUT)
+                bx = psum_plain.tile([P, D_OUT], F32, tag="plain")
+                nc.tensor.matmul(bx[:], lhsT=ident_bf16[:], rhs=bo_in[c][:, cols], start=True, stop=False)
+                nc.tensor.matmul(bx[:], lhsT=ident_bf16[:], rhs=x_in[c][:, cols], start=False, stop=True)
+                nc.scalar.copy(out=o_tiles[c // CHUNKS_PER_BATCH][:, chunk_cols(c, CHUNK_D)][:, cols], in_=bx[:])
+
         def vector_tiles(c):
             return CHUNK_TILES - TT.get(c, 0)
 
@@ -298,14 +307,14 @@ def tile_multiheadattn_pb_t_kernel(tc, h_attn, Wo, bo, x, gamma, beta, out):
                 out=neg_shift[:, b : b + 1], in_=totals[:, :1], func=FUNC.Copy, scale=-1.0 / (P * D_OUT)
             )
 
-        def square_tile(c, j):
+        def square_tile(c, j, width=1):
             b = c // CHUNKS_PER_BATCH
             first = (c % CHUNKS_PER_BATCH) * CHUNK_D + j * D_OUT
             column = stats_column(c, j) + TILES_PER_BATCH
-            squares = scratch_pool.tile([P, D_OUT], BF16)
+            squares = scratch_pool.tile([P, width * D_OUT], BF16)
             nc.scalar.activation(
                 out=squares[:],
-                in_=o_tiles[b][:, first : first + D_OUT],
+                in_=o_tiles[b][:, first : first + width * D_OUT],
                 func=FUNC.Square,
                 bias=neg_shift[:, b : b + 1],
                 accum_out=stats[:, column : column + 1],
@@ -371,8 +380,7 @@ def tile_multiheadattn_pb_t_kernel(tc, h_attn, Wo, bo, x, gamma, beta, out):
             return 0 <= c < CHUNKS
 
         def squares(i):
-            for j in range(CHUNK_TILES):
-                square_tile(i, j)
+            square_tile(i, 0, 4)
 
         whole = slice(0, CHUNK_D)
         halves = [slice(0, CHUNK_D // 2), slice(CHUNK_D // 2, CHUNK_D)]
@@ -400,12 +408,14 @@ def tile_multiheadattn_pb_t_kernel(tc, h_attn, Wo, bo, x, gamma, beta, out):
             for j in range(CHUNK_TILES):
                 project(i, one[j])
                 copy_projection(i, one[j])
-            sum_inputs(i)
             bring(i + 1, 2)
             bring(i + 1, 3)
+            sum_inputs(i)
+            if is_chunk(i + 1):
+                bias_and_residual_on_tensor(i + 1)
             if is_chunk(i + 1):
                 g = GC.get(i + 1, 416)
-                share_bias_and_residual(i + 1, slice(0, g), slice(g - 4, vector_tiles(i + 1) * D_OUT))
+                share_bias_and_residual(i + 1, slice(0, g), slice(g - 4, min(vector_tiles(i + 1), GPSIMD_ADD_TILES) * D_OUT))
             add_projection(i)
             sum_projection(i)
             if i % CHUNKS_PER_BATCH == 0:
@@ -414,8 +424,9 @@ def tile_multiheadattn_pb_t_kernel(tc, h_attn, Wo, bo, x, gamma, beta, out):
             bring(i + 2, 1)
             if i % CHUNKS_PER_BATCH == 0:
                 shift(i // CHUNKS_PER_BATCH)
-            for j in range(CHUNK_TILES):
-                square_tile(i, j)
+            if vector_tiles(i):
+                square_tile(i, 0, vector_tiles(i))
+            square_tile(i, vector_tiles(i), CHUNK_TILES - vector_tiles(i))
             for half in norm_halves(i):
                 normalise_2(half)
             if is_chunk(i + 1):
@@ -486,7 +497,8 @@ def tile_multiheadattn_pb_t_kernel(tc, h_attn, Wo, bo, x, gamma, beta, out):
             for half in halves:
                 normalise_and_store(0, half)
             quantise(3, ALL_TILES)
-            add_bias_and_residual(3, slice(0, vector_tiles(3) * D_OUT))
+            add_bias_and_residual(3, slice(0, 2 * D_OUT))
+            bias_and_residual_on_tensor(3)
             transpose(4, FIRST_HALF)
             for i in range(3, CHUNKS):
                 step(i)

@@ -36,8 +36,8 @@ INPUT_BUFS = 5
 STAGE_BUFS = 3
 
 OTHERS_ADD_FROM = 4
-TT = {3: 1, 4: 1, 5: 2, 6: 2, 7: 2}
-GC = {4: 700, 5: 700, 6: 416, 7: 416}
+TT = {5: 2, 6: 2, 7: 2}
+GC = {4: 832, 5: 832, 6: 416, 7: 416}
 GPSIMD_ADD_TILES = 2
 NORM_LAG = 2
 TENSOR_SUM_TILES = 2
@@ -417,16 +417,14 @@ def tile_multiheadattn_pb_t_kernel(tc, h_attn, Wo, bo, x, gamma, beta, out):
                 g = GC.get(i + 1, 416)
                 share_bias_and_residual(i + 1, slice(0, g), slice(g - 4, min(vector_tiles(i + 1), GPSIMD_ADD_TILES) * D_OUT))
             add_projection(i)
-            sum_projection(i)
             if i % CHUNKS_PER_BATCH == 0:
                 moments(i // CHUNKS_PER_BATCH - 1)
+            sum_projection(i)
             bring(i + 2, 0)
             bring(i + 2, 1)
             if i % CHUNKS_PER_BATCH == 0:
                 shift(i // CHUNKS_PER_BATCH)
-            if vector_tiles(i):
-                square_tile(i, 0, vector_tiles(i))
-            square_tile(i, vector_tiles(i), CHUNK_TILES - vector_tiles(i))
+            squares(i)
             for half in norm_halves(i):
                 normalise_2(half)
             if is_chunk(i + 1):
@@ -462,20 +460,13 @@ def tile_multiheadattn_pb_t_kernel(tc, h_attn, Wo, bo, x, gamma, beta, out):
             add_projection(0)
             shift(0)
             for half in (FIRST_HALF, SECOND_HALF):
-                quantise(1, half)
                 add_bias_and_residual(1, halves[0] if half == FIRST_HALF else halves[1])
-            project(1, slice(0, 1))
-            transpose(2, slice(0, 1))
-            square_tile(0, 0)
-            project(1, slice(1, 2))
-            transpose(2, slice(1, 2))
-            square_tile(0, 1)
-            project(1, slice(2, 3))
-            transpose(2, slice(2, 3))
-            square_tile(0, 2)
-            project(1, slice(3, 4))
-            transpose(2, slice(3, 4))
-            square_tile(0, 3)
+                quantise(1, half)
+            squares(0)
+            project(1, FIRST_HALF)
+            transpose(2, FIRST_HALF)
+            project(1, SECOND_HALF)
+            transpose(2, SECOND_HALF)
             load(5)
             share_bias_and_residual(2, slice(0, 832), slice(828, 1024))
             add_projection(1)

@@ -401,10 +401,13 @@ def tile_multiheadattn_pb_t_kernel(tc, h_attn, Wo, bo, x, gamma, beta, out):
                 if is_chunk(c):
                     transpose(c, one[j])
 
-            for half in norm_halves(i):
-                if half % 4 == 0:
-                    reciprocal(half // 4)
-                normalise_1(half)
+            if i > 4:
+                done = i - 3
+                if done % CHUNKS_PER_BATCH == 0:
+                    reciprocal(done // CHUNKS_PER_BATCH)
+                subtract_mean_and_scale(done, whole)
+            else:
+                normalise_1(i - 1)
             for j in range(CHUNK_TILES):
                 project(i, one[j])
                 copy_projection(i, one[j])
@@ -425,8 +428,10 @@ def tile_multiheadattn_pb_t_kernel(tc, h_attn, Wo, bo, x, gamma, beta, out):
             if i % CHUNKS_PER_BATCH == 0:
                 shift(i // CHUNKS_PER_BATCH)
             squares(i)
-            for half in norm_halves(i):
-                normalise_2(half)
+            if i > 4:
+                normalise_and_store(i - 3, whole)
+            else:
+                normalise_2(i - 1)
             if is_chunk(i + 1):
                 quantise(i + 1, ALL_TILES)
 
@@ -439,11 +444,12 @@ def tile_multiheadattn_pb_t_kernel(tc, h_attn, Wo, bo, x, gamma, beta, out):
             load_bias_and_residual(0, SECOND_HALF)
             load_h(1, ALL_TILES)
             load_bias_and_residual(1)
-            load_h(2, ALL_TILES)
             load_bias_and_residual(2)
+            load_h(2, ALL_TILES)
+            load_bias_and_residual(3)
             nc.sync.dma_start(out=gamma_sb[:], in_=gamma_view)
+            load_h(3, ALL_TILES)
             nc.sync.dma_start(out=beta_sb[:], in_=beta_view)
-            load(3)
             load(4)
             transpose(0, FIRST_HALF)
             regroup_wo(0)
@@ -463,22 +469,21 @@ def tile_multiheadattn_pb_t_kernel(tc, h_attn, Wo, bo, x, gamma, beta, out):
                 add_bias_and_residual(1, halves[0] if half == FIRST_HALF else halves[1])
                 quantise(1, half)
             squares(0)
-            project(1, FIRST_HALF)
-            transpose(2, FIRST_HALF)
-            project(1, SECOND_HALF)
-            transpose(2, SECOND_HALF)
+            project(1, ALL_TILES)
+            transpose(2, ALL_TILES)
             load(5)
             share_bias_and_residual(2, slice(0, 832), slice(828, 1024))
             add_projection(1)
+            add_bias_and_residual(2, halves[1])
             for half in (FIRST_HALF, SECOND_HALF):
                 quantise(2, half)
-            add_bias_and_residual(2, halves[1])
             squares(1)
             project(2, ALL_TILES)
             moments(0)
             transpose(3, ALL_TILES)
             load(6)
             load(7)
+            share_bias_and_residual(3, slice(0, 832), slice(828, 1024))
             add_projection(2)
             shift(1)
             squares(2)
@@ -488,7 +493,6 @@ def tile_multiheadattn_pb_t_kernel(tc, h_attn, Wo, bo, x, gamma, beta, out):
             for half in halves:
                 normalise_and_store(0, half)
             quantise(3, ALL_TILES)
-            add_bias_and_residual(3, slice(0, 2 * D_OUT))
             bias_and_residual_on_tensor(3)
             transpose(4, FIRST_HALF)
             for i in range(3, CHUNKS):

@@ -68,6 +68,7 @@ def tile_multiheadattn_pb_t_kernel(tc, h_attn, Wo, bo, x, gamma, beta, out):
         grouped_pool = ctx.enter_context(tc.tile_pool(name="grouped_pool", bufs=STAGE_BUFS))
         mx_pool = ctx.enter_context(tc.tile_pool(name="mx_pool", bufs=STAGE_BUFS))
         scratch_pool = ctx.enter_context(tc.tile_pool(name="scratch_pool", bufs=1))
+        gpsimd_pool = ctx.enter_context(tc.tile_pool(name="gpsimd_pool", bufs=2))
         sum_pool = ctx.enter_context(tc.tile_pool(name="sum_pool", bufs=2))
         psum_xt = ctx.enter_context(tc.psum_pool(name="psum_xt", bufs=2))
         psum_acc = ctx.enter_context(tc.psum_pool(name="psum_acc", bufs=1))
@@ -123,7 +124,7 @@ def tile_multiheadattn_pb_t_kernel(tc, h_attn, Wo, bo, x, gamma, beta, out):
 
         h_in, bo_in, x_in = {}, {}, {}
         h_grouped, h_codes, h_scales = {}, {}, {}
-        acc_of, total_of = {}, {}
+        acc_of, total_of, shared_sum_of = {}, {}, {}
 
         def chunk_cols(c, width):
             half = c % CHUNKS_PER_BATCH
@@ -161,9 +162,9 @@ def tile_multiheadattn_pb_t_kernel(tc, h_attn, Wo, bo, x, gamma, beta, out):
                     first = j * WORDS + 2 * g * P
                     nc.tensor.transpose(xt[:, a, :], h_words[:, first + u : first + 2 * P : 2], ident[:])
                 nc.scalar.copy(
-                    out=grouped_words[:, j * WORDS : (j + 1) * WORDS].rearrange(
-                        "q (g r u) -> q g r u", g=PASSES, u=2
-                    ),
+                    out=grouped_words.rearrange("q (g j r u) -> q g j r u", g=PASSES, j=CHUNK_TILES, u=2)[:, :, j]
+                    if vector_tiles(c) == 2
+                    else grouped_words[:, j * WORDS : (j + 1) * WORDS].rearrange("q (g r u) -> q g r u", g=PASSES, u=2),
                     in_=xt[:].rearrange("q (g u) r -> q g r u", g=PASSES),
                 )
 
@@ -179,18 +180,22 @@ def tile_multiheadattn_pb_t_kernel(tc, h_attn, Wo, bo, x, gamma, beta, out):
                 in_=h_grouped[c][:, words.start * PACK : words.stop * PACK],
             )
 
+        def tokens_of(c, g, j, tiles=1):
+            first = g * CHUNK_TILES + j if vector_tiles(c) == 2 else j * PASSES + g
+            return slice(first * P, (first + tiles) * P)
+
         def project(c, tiles):
             for j in range(tiles.start, tiles.stop):
                 acc = psum_acc.tile([P, D_OUT], F32, tag="acc%d" % ((j + 2 * c) % CHUNK_TILES))
                 acc_of[(c, j)] = acc
                 if j >= vector_tiles(c):
-                    for f in range(FEATURE_BLOCKS):
-                        block = slice(f * P, (f + 1) * P)
+                    for n in range(2):
+                        f = 2 * (j - 2) + n
                         for g in range(PASSES):
-                            tokens = slice((j * PASSES + g) * P, (j * PASSES + g + 1) * P)
+                            tokens = tokens_of(c, g, 2, 2)
                             features = slice(g * D_OUT + f * P, g * D_OUT + (f + 1) * P)
                             nc.tensor.matmul_mx(
-                                out=acc[:, block],
+                                out=acc[:, n * 2 * P : (n + 1) * 2 * P],
                                 lhsT=wo_codes[:, features].bitcast(FP8X4),
                                 lhsT_scale=wo_scales[:, features],
                                 rhs=h_codes[c][:, tokens].bitcast(FP8X4),
@@ -200,7 +205,7 @@ def tile_multiheadattn_pb_t_kernel(tc, h_attn, Wo, bo, x, gamma, beta, out):
                             )
                     continue
                 for g in range(PASSES):
-                    tokens = slice((j * PASSES + g) * P, (j * PASSES + g + 1) * P)
+                    tokens = tokens_of(c, g, j)
                     features = slice(g * D_OUT, (g + 1) * D_OUT)
                     nc.tensor.matmul_mx(
                         out=acc[:],
@@ -220,11 +225,10 @@ def tile_multiheadattn_pb_t_kernel(tc, h_attn, Wo, bo, x, gamma, beta, out):
             )
 
         def share_bias_and_residual(c, gpsimd_cols, vector_cols):
-            o_chunk = o_tiles[c // CHUNKS_PER_BATCH][:, chunk_cols(c, CHUNK_D)]
+            bx = gpsimd_pool.tile([P, 2 * D_OUT], F32)
             for engine, cols in ((nc.vector, vector_cols), (nc.gpsimd, gpsimd_cols)):
-                engine.tensor_tensor(
-                    out=o_chunk[:, cols], in0=bo_in[c][:, cols], in1=x_in[c][:, cols], op=ADD
-                )
+                engine.tensor_tensor(out=bx[:, cols], in0=bo_in[c][:, cols], in1=x_in[c][:, cols], op=ADD)
+            shared_sum_of[c] = bx
 
         def bias_and_residual_on_tensor(c):
             for j in range(GPSIMD_ADD_TILES, vector_tiles(c)):
@@ -261,7 +265,7 @@ def tile_multiheadattn_pb_t_kernel(tc, h_attn, Wo, bo, x, gamma, beta, out):
                     block = slice(f * P, (f + 1) * P)
                     nc.tensor.matmul(
                         total[:, block],
-                        lhsT=acc_of[(c, j)][:, block],
+                        lhsT=acc_of[(c, 2 + f // 2)][:, ((f % 2) * 2 + j - 2) * P : ((f % 2) * 2 + j - 1) * P],
                         rhs=ident[:],
                         start=False,
                         stop=(f == FEATURE_BLOCKS - 1),
@@ -287,7 +291,7 @@ def tile_multiheadattn_pb_t_kernel(tc, h_attn, Wo, bo, x, gamma, beta, out):
                     out=o_tile,
                     in0=acc_of[(c, j)][:],
                     scalar=0.0,
-                    in1=o_tile,
+                    in1=shared_sum_of[c][:, cols] if c in shared_sum_of and j < 2 else o_tile,
                     op0=ADD,
                     op1=ADD,
                     accum_out=stats[:, column : column + 1],

@@ -188,6 +188,17 @@ def tile_multiheadattn_pb_t_kernel(tc, h_attn, Wo, bo, x, gamma, beta, out):
             for j in range(tiles.start, tiles.stop):
                 acc = psum_acc.tile([P, D_OUT], F32, tag="acc%d" % ((j + 2 * c) % CHUNK_TILES))
                 acc_of[(c, j)] = acc
+                if j == 0 and c > 2:
+                    for n in range(2):
+                        nc.tensor.matmul_mx(
+                            out=acc[:],
+                            lhsT=wo_codes[:, :P].bitcast(FP8X4),
+                            lhsT_scale=wo_scales[:, :P],
+                            rhs=wo_codes[:, :D_OUT].bitcast(FP8X4),
+                            rhs_scale=wo_scales[:, :D_OUT],
+                            start=True,
+                            stop=True,
+                        )
                 if j >= vector_tiles(c):
                     for n in range(2):
                         f = 2 * (j - 2) + n

from contextlib import ExitStack

import concourse.mybir as mybir
from concourse.masks import make_identity

F32 = mybir.dt.float32
BF16 = mybir.dt.bfloat16
U32 = mybir.dt.uint32
U8 = mybir.dt.uint8
FP8X4 = mybir.dt.float8_e4m3fn_x4
ADD = mybir.AluOpType.add
MULT = mybir.AluOpType.mult
FUNC = mybir.ActivationFunctionType

P = 128
BATCH, SEQ, K_DIM, D_OUT = 4, 1024, 1024, 512
LN_EPS = 1e-5
PACK = 4
K_PASS = P * PACK
PASSES = K_DIM // K_PASS
TILES_PER_BATCH = SEQ // P
CHUNK_TILES = 4
CHUNKS_PER_BATCH = TILES_PER_BATCH // CHUNK_TILES
CHUNKS = BATCH * CHUNKS_PER_BATCH
CHUNK_K = CHUNK_TILES * K_DIM
CHUNK_D = CHUNK_TILES * D_OUT
BATCH_D = TILES_PER_BATCH * D_OUT
WORDS = K_DIM // 2
PLANES = WORDS // P
TILE_CODES = K_DIM // PACK
HALF_TILES = CHUNK_TILES // 2
FEATURE_BLOCKS = D_OUT // P
COUNT = SEQ * D_OUT

INPUT_BUFS = 5
STAGE_BUFS = 3

OTHERS_ADD_FROM = 4
TT = {5: 2, 6: 2, 7: 2}
GC = {4: 832, 5: 832, 6: 416, 7: 416}
GPSIMD_ADD_TILES = 2
NORM_LAG = 2
TENSOR_SUM_TILES = 2
G_COLS = 416
TENSOR_NORM_TILES = 2
ALL_TILES = slice(0, CHUNK_TILES)
FIRST_HALF = slice(0, HALF_TILES)
SECOND_HALF = slice(HALF_TILES, CHUNK_TILES)

FLOPS = 2 * BATCH * SEQ * K_DIM * D_OUT


def tile_multiheadattn_pb_t_kernel(tc, h_attn, Wo, bo, x, gamma, beta, out):
    nc = tc.nc

    h_view = h_attn.rearrange("b (p t) k -> p b (t k)", t=TILES_PER_BATCH)
    bo_view = bo.rearrange("b (p t) d -> p b (t d)", t=TILES_PER_BATCH)
    x_view = x.rearrange("b (p t) d -> p b (t d)", t=TILES_PER_BATCH)
    out_view = out.rearrange("b (p t) d -> p b (t d)", t=TILES_PER_BATCH)
    gamma_view = gamma.rearrange("(p t) d -> p (t d)", t=TILES_PER_BATCH)
    beta_view = beta.rearrange("(p t) d -> p (t d)", t=TILES_PER_BATCH)
    wo_view = Wo.rearrange("(g q t) c -> q g (t c)", g=PASSES, t=PACK)

    with ExitStack() as ctx:
        const = ctx.enter_context(tc.tile_pool(name="const", bufs=1))
        h_pool = ctx.enter_context(tc.tile_pool(name="h_pool", bufs=INPUT_BUFS))
        add_pool = ctx.enter_context(tc.tile_pool(name="add_pool", bufs=INPUT_BUFS))
        grouped_pool = ctx.enter_context(tc.tile_pool(name="grouped_pool", bufs=STAGE_BUFS))
        mx_pool = ctx.enter_context(tc.tile_pool(name="mx_pool", bufs=STAGE_BUFS))
        scratch_pool = ctx.enter_context(tc.tile_pool(name="scratch_pool", bufs=1))
        gpsimd_pool = ctx.enter_context(tc.tile_pool(name="gpsimd_pool", bufs=2))
        sum_pool = ctx.enter_context(tc.tile_pool(name="sum_pool", bufs=2))
        psum_xt = ctx.enter_context(tc.psum_pool(name="psum_xt", bufs=2))
        psum_acc = ctx.enter_context(tc.psum_pool(name="psum_acc", bufs=1))
        psum_plain = ctx.enter_context(tc.psum_pool(name="psum_plain", bufs=2))

        ident = const.tile([P, P], F32)
        make_identity(nc, ident[:])
        ident_bf16 = const.tile([P, P], BF16)
        make_identity(nc, ident_bf16[:])
        ones = const.tile([P, P], F32)
        nc.vector.memset(ones[:], 1.0)
        eps_part = const.tile([P, 1], F32)
        nc.vector.memset(eps_part[:], LN_EPS / TILES_PER_BATCH)

        STATS = 2 * TILES_PER_BATCH
        stats = const.tile([P, BATCH * STATS], F32)
        nc.vector.memset(stats[:], 0.0)
        scratch = const.tile([P, BATCH * STATS], F32)
        neg_shift = const.tile([P, BATCH], F32)
        neg_mean = const.tile([P, BATCH], F32)
        mean_square = const.tile([P, BATCH], F32)
        gap_square = const.tile([P, BATCH], F32)
        std = const.tile([P, BATCH], F32)
        rstd = const.tile([P, BATCH], F32)

        nc.scalar.activation(out=std[:, :1], in_=eps_part[:], func=FUNC.Sqrt)

        o_tiles = [const.tile([P, BATCH_D], F32, name="o%d" % b) for b in range(BATCH)]
        gamma_sb = const.tile([P, BATCH_D], BF16)
        beta_sb = const.tile([P, BATCH_D], BF16)
        diagonal = const.tile([P, P], F32)

        wo_raw = const.tile([P, PASSES * PACK * D_OUT], BF16)
        wo_grouped = const.tile([P, PASSES * D_OUT * PACK], BF16, align_bytes=64)
        wo_codes = const.tile([P, PASSES * D_OUT], U32, align_bytes=64)
        wo_scales = const.tile([P, PASSES * D_OUT], U8, align_bytes=64)
        wo_raw_passes = wo_raw[:].rearrange("q (g r) -> q g r", g=PASSES)
        wo_raw_cti = wo_raw[:].rearrange("q (g t c i) -> q g c t i", g=PASSES, t=PACK, i=4)
        wo_grouped_cti = wo_grouped[:].rearrange("q (g c i t) -> q g c t i", g=PASSES, i=4, t=PACK)

        def load_wo(g):
            nc.sync.dma_start(out=wo_raw_passes[:, g, :], in_=wo_view[:, g, :])

        def regroup_wo(g):
            nc.vector.tensor_copy(out=wo_grouped_cti[:, g], in_=wo_raw_cti[:, g])

        def quantise_wo(g):
            nc.vector.quantize_mx(
                out=wo_codes[:, g * D_OUT : (g + 1) * D_OUT].bitcast(FP8X4),
                scales=wo_scales[:, g * D_OUT : (g + 1) * D_OUT],
                in_=wo_grouped[:, g * D_OUT * PACK : (g + 1) * D_OUT * PACK],
            )

        h_in, bo_in, x_in = {}, {}, {}
        h_grouped, h_codes, h_scales = {}, {}, {}
        acc_of, total_of, shared_sum_of = {}, {}, {}

        def chunk_cols(c, width):
            half = c % CHUNKS_PER_BATCH
            return slice(half * width, (half + 1) * width)

        def load_h(c, tiles):
            if tiles.start == 0:
                h_in[c] = h_pool.tile([P, CHUNK_K], BF16, name="h_sb")
            cols = slice(tiles.start * K_DIM, tiles.stop * K_DIM)
            chunk = h_view[:, c // CHUNKS_PER_BATCH, chunk_cols(c, CHUNK_K)]
            nc.sync.dma_start(out=h_in[c][:, cols], in_=chunk[:, cols])

        def load_bias_and_residual(c, tiles=ALL_TILES):
            if tiles.start == 0:
                bo_in[c] = add_pool.tile([P, CHUNK_D], BF16, name="bo_sb")
                x_in[c] = add_pool.tile([P, CHUNK_D], BF16, name="x_sb")
            cols = slice(tiles.start * D_OUT, tiles.stop * D_OUT)
            for view, tile in ((bo_view, bo_in[c]), (x_view, x_in[c])):
                chunk = view[:, c // CHUNKS_PER_BATCH, chunk_cols(c, CHUNK_D)]
                nc.sync.dma_start(out=tile[:, cols], in_=chunk[:, cols])

        def load(c):
            load_h(c, ALL_TILES)
            load_bias_and_residual(c)

        def transpose(c, tiles):
            if tiles.start == 0:
                h_grouped[c] = grouped_pool.tile([P, CHUNK_K], BF16, align_bytes=64, name="grouped")
            h_words = h_in[c][:].bitcast(F32)
            grouped_words = h_grouped[c][:].bitcast(F32)
            for j in range(tiles.start, tiles.stop):
                xt = psum_xt.tile([P, PLANES, P], F32)
                for a in range(PLANES):
                    g, u = divmod(a, 2)
                    first = j * WORDS + 2 * g * P
                    nc.tensor.transpose(xt[:, a, :], h_words[:, first + u : first + 2 * P : 2], ident[:])
                nc.scalar.copy(
                    out=grouped_words.rearrange("q (g j r u) -> q g j r u", g=PASSES, j=CHUNK_TILES, u=2)[:, :, j]
                    if vector_tiles(c) == 2
                    else grouped_words[:, j * WORDS : (j + 1) * WORDS].rearrange("q (g r u) -> q g r u", g=PASSES, u=2),
                    in_=xt[:].rearrange("q (g u) r -> q g r u", g=PASSES),
                )

        def quantise(c, tiles):
            if tiles.start == 0:
                width = CHUNK_TILES * TILE_CODES
                h_codes[c] = mx_pool.tile([P, width], U32, align_bytes=64, name="codes")
                h_scales[c] = mx_pool.tile([P, width], U8, align_bytes=64, name="scales")
            words = slice(tiles.start * TILE_CODES, tiles.stop * TILE_CODES)
            nc.vector.quantize_mx(
                out=h_codes[c][:, words].bitcast(FP8X4),
                scales=h_scales[c][:, words],
                in_=h_grouped[c][:, words.start * PACK : words.stop * PACK],
            )

        def tokens_of(c, g, j, tiles=1):
            first = g * CHUNK_TILES + j if vector_tiles(c) == 2 else j * PASSES + g
            return slice(first * P, (first + tiles) * P)

        def project(c, tiles):
            for j in range(tiles.start, tiles.stop):
                acc = psum_acc.tile([P, D_OUT], F32, tag="acc%d" % ((j + 2 * c) % CHUNK_TILES))
                acc_of[(c, j)] = acc
                if j == 0 and c > 2:
                    for n in range(2):
                        nc.tensor.matmul_mx(
                            out=acc[:],
                            lhsT=wo_codes[:, :P].bitcast(FP8X4),
                            lhsT_scale=wo_scales[:, :P],
                            rhs=wo_codes[:, :D_OUT].bitcast(FP8X4),
                            rhs_scale=wo_scales[:, :D_OUT],
                            start=True,
                            stop=True,
                        )
                if j >= vector_tiles(c):
                    for n in range(2):
                        f = 2 * (j - 2) + n
                        for g in range(PASSES):
                            tokens = tokens_of(c, g, 2, 2)
                            features = slice(g * D_OUT + f * P, g * D_OUT + (f + 1) * P)
                            nc.tensor.matmul_mx(
                                out=acc[:, n * 2 * P : (n + 1) * 2 * P],
                                lhsT=wo_codes[:, features].bitcast(FP8X4),
                                lhsT_scale=wo_scales[:, features],
                                rhs=h_codes[c][:, tokens].bitcast(FP8X4),
                                rhs_scale=h_scales[c][:, tokens],
                                start=(g == 0),
                                stop=(g == PASSES - 1),
                            )
                    continue
                for g in range(PASSES):
                    tokens = tokens_of(c, g, j)
                    features = slice(g * D_OUT, (g + 1) * D_OUT)
                    nc.tensor.matmul_mx(
                        out=acc[:],
                        lhsT=h_codes[c][:, tokens].bitcast(FP8X4),
                        lhsT_scale=h_scales[c][:, tokens],
                        rhs=wo_codes[:, features].bitcast(FP8X4),
                        rhs_scale=wo_scales[:, features],
                        start=(g == 0),
                        stop=(g == PASSES - 1),
                    )

        def add_bias_and_residual(c, cols):
            engine_of = nc.vector
            o_chunk = o_tiles[c // CHUNKS_PER_BATCH][:, chunk_cols(c, CHUNK_D)]
            engine_of.tensor_tensor(
                out=o_chunk[:, cols], in0=bo_in[c][:, cols], in1=x_in[c][:, cols], op=ADD
            )

        def share_bias_and_residual(c, gpsimd_cols, vector_cols):
            bx = gpsimd_pool.tile([P, 2 * D_OUT], F32)
            for engine, cols in ((nc.vector, vector_cols), (nc.gpsimd, gpsimd_cols)):
                engine.tensor_tensor(out=bx[:, cols], in0=bo_in[c][:, cols], in1=x_in[c][:, cols], op=ADD)
            shared_sum_of[c] = bx

        def bias_and_residual_on_tensor(c):
            for j in range(GPSIMD_ADD_TILES, vector_tiles(c)):
                cols = slice(j * D_OUT, (j + 1) * D_OUT)
                bx = psum_plain.tile([P, D_OUT], F32, tag="plain")
                nc.tensor.matmul(bx[:], lhsT=ident_bf16[:], rhs=bo_in[c][:, cols], start=True, stop=False)
                nc.tensor.matmul(bx[:], lhsT=ident_bf16[:], rhs=x_in[c][:, cols], start=False, stop=True)
                nc.scalar.copy(out=o_tiles[c // CHUNKS_PER_BATCH][:, chunk_cols(c, CHUNK_D)][:, cols], in_=bx[:])

        def vector_tiles(c):
            return CHUNK_TILES - TT.get(c, 0)

        def copy_projection(c, tiles=ALL_TILES):
            for j in range(max(tiles.start, vector_tiles(c)), tiles.stop):
                acc_sb = sum_pool.tile([P, D_OUT], F32)
                nc.scalar.copy(out=acc_sb[:], in_=acc_of[(c, j)][:])
                acc_of[(c, j)] = acc_sb

        def sum_inputs(c):
            for j in range(vector_tiles(c), CHUNK_TILES):
                cols = slice(j * D_OUT, (j + 1) * D_OUT)
                total = psum_plain.tile([P, D_OUT], F32, tag="plain")
                nc.tensor.matmul(total[:], lhsT=ident_bf16[:], rhs=bo_in[c][:, cols], start=True, stop=False)
                nc.tensor.matmul(total[:], lhsT=ident_bf16[:], rhs=x_in[c][:, cols], start=False, stop=False)
                total_of[(c, j)] = total

        def sum_projection(c):
            o_chunk = o_tiles[c // CHUNKS_PER_BATCH][:, chunk_cols(c, CHUNK_D)]
            for j in range(vector_tiles(c), CHUNK_TILES):
                cols = slice(j * D_OUT, (j + 1) * D_OUT)
                column = stats_column(c, j)
                total = total_of[(c, j)]
                for f in range(FEATURE_BLOCKS):
                    block = slice(f * P, (f + 1) * P)
                    nc.tensor.matmul(
                        total[:, block],
                        lhsT=acc_of[(c, 2 + f // 2)][:, ((f % 2) * 2 + j - 2) * P : ((f % 2) * 2 + j - 1) * P],
                        rhs=ident[:],
                        start=False,
                        stop=(f == FEATURE_BLOCKS - 1),
                        is_transpose=True,
                    )
                nc.scalar.activation(
                    out=o_chunk[:, cols],
                    in_=total[:],
                    func=FUNC.Copy,
                    accum_out=stats[:, column : column + 1],
                )

        def stats_column(c, j):
            return (c // CHUNKS_PER_BATCH) * STATS + (c % CHUNKS_PER_BATCH) * CHUNK_TILES + j

        def add_projection(c):
            o_chunk = o_tiles[c // CHUNKS_PER_BATCH][:, chunk_cols(c, CHUNK_D)]
            for j in range(vector_tiles(c)):
                cols = slice(j * D_OUT, (j + 1) * D_OUT)
                o_tile = o_chunk[:, cols]
                column = stats_column(c, j)
                nc.vector.scalar_tensor_tensor(
                    out=o_tile,
                    in0=acc_of[(c, j)][:],
                    scalar=0.0,
                    in1=shared_sum_of[c][:, cols] if c in shared_sum_of and j < 2 else o_tile,
                    op0=ADD,
                    op1=ADD,
                    accum_out=stats[:, column : column + 1],
                )

        def totals_of(first, width):
            totals = psum_xt.tile([P, STATS], F32, tag="xt")
            nc.tensor.matmul(
                totals[:, :width], lhsT=ones[:], rhs=stats[:, first : first + width], start=True, stop=True
            )
            return totals

        def shift(b):
            first = stats_column(b * CHUNKS_PER_BATCH, 0)
            totals = totals_of(first, 1)
            nc.scalar.activation(
                out=neg_shift[:, b : b + 1], in_=totals[:, :1], func=FUNC.Copy, scale=-1.0 / (P * D_OUT)
            )

        def square_tile(c, j, width=1):
            b = c // CHUNKS_PER_BATCH
            first = (c % CHUNKS_PER_BATCH) * CHUNK_D + j * D_OUT
            column = stats_column(c, j) + TILES_PER_BATCH
            squares = scratch_pool.tile([P, width * D_OUT], BF16)
            nc.scalar.activation(
                out=squares[:],
                in_=o_tiles[b][:, first : first + width * D_OUT],
                func=FUNC.Square,
                bias=neg_shift[:, b : b + 1],
                accum_out=stats[:, column : column + 1],
            )

        def moments(b):
            first = b * STATS
            middle = first + TILES_PER_BATCH
            totals = totals_of(first, STATS)
            nc.scalar.activation(
                out=scratch[:, first:middle],
                in_=totals[:, :TILES_PER_BATCH],
                func=FUNC.Copy,
                scale=-1.0 / COUNT,
                accum_out=neg_mean[:, b : b + 1],
            )
            nc.scalar.activation(
                out=scratch[:, middle : first + STATS],
                in_=totals[:, TILES_PER_BATCH:],
                func=FUNC.Identity,
                scale=1.0 / COUNT,
                bias=eps_part[:],
                accum_out=mean_square[:, b : b + 1],
            )
            nc.scalar.activation(
                out=gap_square[:, b : b + 1],
                in_=neg_mean[:, b : b + 1],
                func=FUNC.Square,
                scale=-1.0,
                bias=neg_shift[:, b : b + 1],
            )
            nc.scalar.activation(
                out=std[:, b : b + 1],
                in_=gap_square[:, b : b + 1],
                func=FUNC.Sqrt,
                scale=-1.0,
                bias=mean_square[:, b : b + 1],
            )

        def reciprocal(b):
            nc.vector.reciprocal(out=rstd[:, b : b + 1], in_=std[:, b : b + 1])

        def part_of(c, part):
            b = c // CHUNKS_PER_BATCH
            first = (c % CHUNKS_PER_BATCH) * CHUNK_D
            cols = slice(first + part.start, first + part.stop)
            return b, o_tiles[b][:, cols], cols

        def subtract_mean_and_scale(c, part):
            b, o, cols = part_of(c, part)
            nc.vector.scalar_tensor_tensor(
                out=o, in0=o, scalar=neg_mean[:, b : b + 1], in1=gamma_sb[:, cols], op0=ADD, op1=MULT
            )

        def normalise_and_store(c, part):
            b, o, cols = part_of(c, part)
            nc.vector.scalar_tensor_tensor(
                out=o, in0=o, scalar=rstd[:, b : b + 1], in1=beta_sb[:, cols], op0=MULT, op1=ADD
            )
            nc.sync.dma_start(out=out_view[:, b, cols], in_=o)

        def is_chunk(c):
            return 0 <= c < CHUNKS

        def squares(i):
            square_tile(i, 0, 4)

        whole = slice(0, CHUNK_D)
        halves = [slice(0, CHUNK_D // 2), slice(CHUNK_D // 2, CHUNK_D)]

        def normalise_1(half):
            subtract_mean_and_scale(half // 2, halves[half % 2])

        def normalise_2(half):
            normalise_and_store(half // 2, halves[half % 2])

        def norm_halves(i):
            return [i - 1] if i < 5 else [2 * i - 6, 2 * i - 5]

        def step(i):
            one = [slice(j, j + 1) for j in range(CHUNK_TILES)]

            def bring(c, j):
                if is_chunk(c):
                    transpose(c, one[j])

            if i > 4:
                done = i - 3
                if done % CHUNKS_PER_BATCH == 0:
                    reciprocal(done // CHUNKS_PER_BATCH)
                subtract_mean_and_scale(done, whole)
            else:
                normalise_1(i - 1)
            for j in range(CHUNK_TILES):
                project(i, one[j])
                copy_projection(i, one[j])
            bring(i + 1, 2)
            bring(i + 1, 3)
            sum_inputs(i)
            if is_chunk(i + 1):
                bias_and_residual_on_tensor(i + 1)
            if is_chunk(i + 1):
                g = GC.get(i + 1, 416)
                share_bias_and_residual(i + 1, slice(0, g), slice(g - 4, min(vector_tiles(i + 1), GPSIMD_ADD_TILES) * D_OUT))
            add_projection(i)
            if i % CHUNKS_PER_BATCH == 0:
                moments(i // CHUNKS_PER_BATCH - 1)
            sum_projection(i)
            bring(i + 2, 0)
            bring(i + 2, 1)
            if i % CHUNKS_PER_BATCH == 0:
                shift(i // CHUNKS_PER_BATCH)
            squares(i)
            if i > 4:
                normalise_and_store(i - 3, whole)
            else:
                normalise_2(i - 1)
            if is_chunk(i + 1):
                quantise(i + 1, ALL_TILES)

        with tc.manual_schedule():
            load_h(0, FIRST_HALF)
            load_wo(0)
            load_wo(1)
            load_bias_and_residual(0, FIRST_HALF)
            load_h(0, SECOND_HALF)
            load_bias_and_residual(0, SECOND_HALF)
            load_h(1, ALL_TILES)
            load_bias_and_residual(1)
            load_bias_and_residual(2)
            load_h(2, ALL_TILES)
            load_bias_and_residual(3)
            nc.sync.dma_start(out=gamma_sb[:], in_=gamma_view)
            load_h(3, ALL_TILES)
            nc.sync.dma_start(out=beta_sb[:], in_=beta_view)
            load(4)
            transpose(0, FIRST_HALF)
            regroup_wo(0)
            quantise(0, FIRST_HALF)
            nc.scalar.copy(out=wo_grouped_cti[:, 1], in_=wo_raw_cti[:, 1])
            quantise_wo(0)
            add_bias_and_residual(0, slice(0, 1024))
            quantise_wo(1)
            transpose(0, SECOND_HALF)
            add_bias_and_residual(0, slice(1024, 2048))
            quantise(0, SECOND_HALF)
            project(0, ALL_TILES)
            transpose(1, ALL_TILES)
            add_projection(0)
            shift(0)
            for half in (FIRST_HALF, SECOND_HALF):
                add_bias_and_residual(1, halves[0] if half == FIRST_HALF else halves[1])
                quantise(1, half)
            squares(0)
            project(1, ALL_TILES)
            transpose(2, ALL_TILES)
            load(5)
            share_bias_and_residual(2, slice(0, 832), slice(828, 1024))
            add_projection(1)
            add_bias_and_residual(2, halves[1])
            for half in (FIRST_HALF, SECOND_HALF):
                quantise(2, half)
            squares(1)
            project(2, ALL_TILES)
            moments(0)
            transpose(3, ALL_TILES)
            load(6)
            load(7)
            share_bias_and_residual(3, slice(0, 832), slice(828, 1024))
            add_projection(2)
            shift(1)
            squares(2)
            reciprocal(0)
            for half in halves:
                subtract_mean_and_scale(0, half)
            for half in halves:
                normalise_and_store(0, half)
            quantise(3, ALL_TILES)
            bias_and_residual_on_tensor(3)
            transpose(4, FIRST_HALF)
            for i in range(3, CHUNKS):
                step(i)
            moments(BATCH - 1)
            for half in (10, 11):
                normalise_1(half)
            for half in (10, 11):
                normalise_2(half)
            b, c = BATCH - 1, CHUNKS - 1
            tiles = [slice(j * D_OUT, (j + 1) * D_OUT) for j in range(CHUNK_TILES)]
            shared = tiles[CHUNK_TILES - TENSOR_NORM_TILES :]
            own = [(c - 1, tile) for tile in tiles] + [(c, tile) for tile in tiles if tile not in shared]
            reciprocal(b)
            nc.scalar.activation(out=diagonal[:], in_=ident[:], func=FUNC.Copy, scale=rstd[:, b : b + 1])
            for tile in shared:
                subtract_mean_and_scale(c, tile)
            for tile in shared:
                o, cols = part_of(c, tile)[1:]
                total = psum_acc.tile([P, D_OUT], F32, tag="acc%d" % (cols.start // D_OUT % CHUNK_TILES))
                nc.tensor.matmul(total[:], lhsT=diagonal[:], rhs=o, start=True, stop=False)
                nc.tensor.matmul(total[:], lhsT=ident_bf16[:], rhs=beta_sb[:, cols], start=False, stop=True)
                nc.scalar.copy(out=o, in_=total[:])
            for n in range(0, len(own), 2):
                for piece in own[n : n + 2]:
                    subtract_mean_and_scale(*piece)
                for piece in own[n : n + 2]:
                    normalise_and_store(*piece)
                if n == 2:
                    o, cols = part_of(c, slice(shared[0].start, shared[-1].stop))[1:]
                    nc.sync.dma_start(out=out_view[:, b, cols], in_=o)
